import numpy as np
import ml_dtypes


def mxq(x, axis, fmt="e4m3"):
    dtype, down = {"e4m3": (ml_dtypes.float8_e4m3fn, 7), "e5m2": (ml_dtypes.float8_e5m2, 14)}[fmt]
    v = np.moveaxis(np.asarray(x, np.float32).astype(ml_dtypes.bfloat16).astype(np.float64), axis, -1)
    blocks = v.reshape(v.shape[:-1] + (-1, 32))
    amax = np.abs(blocks).max(-1, keepdims=True)
    byte = np.maximum(np.where(amax > 0, np.frexp(amax)[1] - 1 + 127, 0) - down, 1)
    scale = np.exp2(byte - 127.0)
    codes = (blocks / scale).astype(np.float32).astype(dtype).astype(np.float64)
    return np.moveaxis((codes * scale).reshape(v.shape), -1, axis)


WIDE = False


def mx_kscale(k):
    if not WIDE:
        return np.ones(k)
    levels = np.array([10, -10, 5, -5, 0])
    a = np.random.permutation(np.resize(levels, k // 512 * 4)).reshape(k // 512, 4)
    idx = np.arange(k)
    return np.exp2(a[idx // 512, idx % 128 // 32])


BF16 = ml_dtypes.bfloat16


def bf(x):
    return np.asarray(x, np.float32).astype(BF16)


def f64(x):
    return np.asarray(x).astype(np.float64)


E2M1 = np.array([0.0, 0.5, 1.0, 1.5, 2.0, 3.0, 4.0, 6.0, -0.0, -0.5, -1.0, -1.5, -2.0, -3.0, -4.0, -6.0])


def pack_weight(w, fmt):
    k, n = w.shape
    w = f64(bf(w)).reshape(k // 32, 32, n)
    amax = np.abs(w).max(1)
    if fmt == "e4m3":
        byte = np.frexp(amax)[1] - 1 + 127 - 7
    else:
        mant, ex = np.frexp(amax / 6.0)
        byte = np.where(mant > 0.5, ex, ex - 1) + 127
    byte = np.clip(np.where(amax > 0, byte, 1), 1, 254)
    scaled = (w * np.exp2(127.0 - byte)[:, None, :]).reshape(k, n).astype(np.float32)
    by_word = np.ascontiguousarray(scaled.reshape(k // 512, 128, 4, n).transpose(0, 1, 3, 2))
    if fmt == "e4m3":
        words = by_word.astype(ml_dtypes.float8_e4m3fn).view(np.uint8)
    else:
        c = by_word.astype(ml_dtypes.float4_e2m1fn).view(np.uint8) & 0xF
        words = c[..., 0::2] | (c[..., 1::2] << 4)
    return np.ascontiguousarray(words), np.ascontiguousarray(byte.astype(np.uint8).reshape(k // 512, 16, n))


def unpack_weight(words, scales, fmt):
    g, p, n, _ = words.shape
    if fmt == "e4m3":
        vals = np.ascontiguousarray(words).view(ml_dtypes.float8_e4m3fn).astype(np.float64)
    else:
        nib = np.empty((g, p, n, 4), np.uint8)
        nib[..., 0::2] = words & 0xF
        nib[..., 1::2] = words >> 4
        vals = E2M1[nib]
    vals = vals * np.repeat(np.exp2(scales.astype(np.float64) - 127.0), 8, axis=1)[..., None]
    return vals.transpose(0, 1, 3, 2).reshape(g * 512, n)

def pack4(w):
    words, scales = pack_weight(w, "e2m1")
    return words.reshape(words.shape[0], 128, -1), scales


def unpack4(words, scales):
    return unpack_weight(words.reshape(words.shape[0], 128, -1, 2), scales, "e2m1")


GRID_MIN, GRID_MAX = -2.0, 2.0
NUM_GRIDS = 8
NUM_KNOTS = NUM_GRIDS + 1
IN_F, OUT_F = 1024, 1024
BATCH = 512


def silu(v):
    with np.errstate(over="ignore"):
        return v / (1.0 + np.exp(-v))


def setup_inputs():
    s = mx_kscale(IN_F)
    bound_base = np.sqrt(6.0 / ((1 + 5) * IN_F))
    x = bf(np.random.standard_normal((BATCH, IN_F)) * s)
    spline_weight = bf(np.random.standard_normal((OUT_F, IN_F, NUM_KNOTS)) * 0.02)
    base_weight = np.random.uniform(-bound_base, bound_base, (OUT_F, IN_F)) / s
    words, scales = pack4(np.ascontiguousarray(base_weight.T))
    bias = bf(np.random.standard_normal(OUT_F) * 0.3)
    return {"x": x,
            "spline_weight": spline_weight,
            "base_weight_words": words,
            "base_weight_scales": scales,
            "bias": bias}


def reference(x, spline_weight, base_weight_words, base_weight_scales, bias):
    x = f64(x)
    grid = np.linspace(GRID_MIN, GRID_MAX, NUM_KNOTS)
    delta = (GRID_MAX - GRID_MIN) / NUM_GRIDS
    xc = np.clip(x, GRID_MIN, GRID_MAX)
    basis = np.maximum(1.0 - np.abs((xc[..., None] - grid) / delta), 0.0)
    bq = mxq(basis.transpose(2, 0, 1), 2, "e4m3")
    wq = mxq(f64(spline_weight).transpose(2, 1, 0), 1, "e4m3")
    out = (bq @ wq).sum(0)
    out = out + (mxq(silu(x), 1, "e4m3") @ unpack4(base_weight_words, base_weight_scales))
    return out + f64(bias)

@@ -1,0 +1,280 @@
+from contextlib import ExitStack
+
+import concourse.mybir as mybir
+from concourse.masks import make_identity
+
+F32 = mybir.dt.float32
+BF16 = mybir.dt.bfloat16
+I32 = mybir.dt.int32
+U32 = mybir.dt.uint32
+U8 = mybir.dt.uint8
+FP8X4 = mybir.dt.float8_e4m3fn_x4
+FP4X4 = mybir.dt.float4_e2m1fn_x4
+ALU = mybir.AluOpType
+AF = mybir.ActivationFunctionType
+
+FLOPS = 2 * 512 * 1024 * 1024 * 10
+
+P = 128
+NT = 8
+NR = 9
+MANUAL = False
+NA = 4
+NTP = 8 - NA
+NW = 5
+GB = 3
+BQ = 2
+NG = 8
+
+
+def tile_kanbasislinear_kernel(tc, x, spline_weight, base_weight_words, base_weight_scales, bias, out):
+    nc = tc.nc
+    with ExitStack() as ctx:
+        const = ctx.enter_context(tc.tile_pool(name="const", bufs=1))
+        work = ctx.enter_context(tc.tile_pool(name="work", bufs=1))
+        wnat = ctx.enter_context(tc.tile_pool(name="wnat", bufs=2))
+        gpool = ctx.enter_context(tc.tile_pool(name="gpool", bufs=NG))
+        cpool = ctx.enter_context(tc.tile_pool(name="cpool", bufs=NW))
+        opool = ctx.enter_context(tc.tile_pool(name="opool", bufs=2))
+        psum = ctx.enter_context(tc.psum_pool(name="psum", bufs=1))
+        if MANUAL:
+            ctx.enter_context(tc.manual_schedule())
+
+        def bank(name):
+            return psum.tile([P, 512], F32, tag="tp", bufs=NTP, name=name)
+
+        warm = const.tile([P, 2], F32, name="warm")
+        nc.vector.memset(warm[:], 0.0)
+        nc.scalar.activation(out=warm[:, 1:2], in_=warm[:, 0:1], func=AF.Silu)
+        x_sb = work.tile([P, 4, 1024], BF16, tag="bg", bufs=2, name="x_sb", align_bytes=64)
+        nc.sync.dma_start(out=x_sb[:], in_=x.rearrange("(t p) i -> p t i", p=P))
+        ident_f = const.tile([P, P], F32, name="ident_f")
+        make_identity(nc, ident_f[:])
+        ident_b = const.tile([P, P], BF16, name="ident_b")
+        make_identity(nc, ident_b[:])
+        brow = const.tile([P, P], BF16, name="brow")
+        nc.vector.memset(brow[:], 0.0)
+        bs = const.tile([P, 2, 1024], U8, name="bs", align_bytes=64)
+        nc.vector.memset(bs[:].bitcast(I32), 0)
+        bw = const.tile([P, 2, 2048], U8, name="bw", align_bytes=64)
+
+        wn = {}
+
+        def load_w(t):
+            wn[t] = wnat.tile([P, 9216], BF16, tag="wn", name="wn")
+            nc.sync.dma_start(out=wn[t][:], in_=spline_weight[P * t:P * t + P].rearrange("o i k -> o (i k)"))
+
+        load_w(0)
+        nc.sync.dma_start(out=brow[0:8, :], in_=bias.rearrange("(t p) -> t p", p=P))
+        sc_rows = base_weight_scales.rearrange("g q n -> q g n")
+        for r in range(4):
+            nc.sync.dma_start(out=bs[r:P:32, :, :].bitcast(I32), in_=sc_rows[r:16:4].bitcast(I32))
+        nc.sync.dma_start(out=bw[:].bitcast(I32), in_=base_weight_words.rearrange("g p n -> p g n").bitcast(I32))
+        load_w(1)
+
+        xw = x_sb[:].bitcast(F32)
+        xp = work.tile([P, 2, 512, 4], BF16, tag="ra", name="xp")
+        for bt in range(4):
+            tpx = bank("tpx")
+            for u in range(4):
+                nc.tensor.transpose(tpx[:, P * u:P * u + P], xw[:, bt, u:512:4], ident_f[:])
+            src = tpx[:].bitcast(BF16).rearrange("p (u b e) -> p e b u", u=4, b=P, e=2)
+            dst = xp[:, :, P * bt:P * bt + P, :]
+            if bt % 2 == 0:
+                nc.scalar.activation(out=dst, in_=src, func=AF.Copy, scale=2.0)
+            else:
+                nc.vector.tensor_scalar(out=dst, in0=src, scalar1=2.0, scalar2=None, op0=ALU.mult)
+        xs = const.tile([P, 4096], BF16, name="xs")
+        nxs = const.tile([P, 4096], BF16, name="nxs")
+        nc.vector.tensor_scalar(out=xs[:], in0=xp[:].rearrange("p h b u -> p (h b u)"), scalar1=-4.0, scalar2=4.0,
+                                op0=ALU.max, op1=ALU.min)
+        nc.vector.tensor_scalar(out=nxs[:], in0=xs[:], scalar1=-1.0, scalar2=None, op0=ALU.mult)
+
+        sg = work.tile([P, 2, 512, 4], BF16, tag="bg", bufs=2, name="sg", align_bytes=64)
+        for bt in range(4):
+            tps = bank("tps")
+            for g in range(2):
+                for u in range(2):
+                    nc.tensor.transpose(tps[:, P * (2 * g + u):P * (2 * g + u) + P],
+                                        xw[:, bt, 256 * g + u:256 * (g + 1):2], ident_f[:])
+            v = tps[:].bitcast(BF16).rearrange("p (g u b e) -> p g b u e", g=2, u=2, b=P, e=2)
+            for g in range(2):
+                nc.scalar.activation(out=sg[:, g, P * bt:P * bt + P, :].rearrange("p b (u e) -> p b u e", u=2, e=2),
+                                     in_=v[:, g], func=AF.Silu)
+        tpb = psum.tile([P, P], BF16, tag="tp", bufs=NTP, name="tpb")
+        nc.tensor.transpose(tpb[:], brow[:], ident_b[:])
+        bcol = const.tile([P, 8], F32, name="bcol")
+        nc.vector.tensor_copy(out=bcol[:], in_=tpb[:, 0:8])
+        scod = const.tile([P, 1024], U32, name="scod", align_bytes=64)
+        ssc = const.tile([P, 1024], U8, name="ssc", align_bytes=64)
+        nc.vector.quantize_mx(out=scod[:].bitcast(FP8X4), scales=ssc[:], in_=sg[:].rearrange("p g b t -> p (g b t)"))
+
+        bc = const.tile([P, 9, 1024], U32, name="bc", align_bytes=64)
+        bsc = const.tile([P, 9, 1024], U8, name="bsc", align_bytes=64)
+        tmp = {}
+
+        def new_bg(k):
+            tmp["g", k] = work.tile([P, 4096], BF16, tag="bg", bufs=2, name="bg", align_bytes=64)
+            return tmp["g", k]
+
+        def ramp(dst, src, shift):
+            nc.vector.tensor_scalar(out=dst[:], in0=src[:], scalar1=float(shift), scalar2=0.0, op0=ALU.add, op1=ALU.max)
+
+        def piece(kind, k):
+            if kind == "a":
+                if k == 0:
+                    ramp(new_bg(k), nxs, -3)
+                elif k == 8:
+                    ramp(new_bg(k), xs, -3)
+                else:
+                    tmp["a"] = work.tile([P, 4096], BF16, tag="ra", name="ra")
+                    ramp(tmp["a"], xs, 5 - k)
+            elif kind == "b":
+                tmp["b"] = work.tile([P, 4096], BF16, tag="rb", name="rb")
+                ramp(tmp["b"], nxs, k - 3)
+            elif kind == "m":
+                nc.vector.tensor_tensor(out=new_bg(k)[:], in0=tmp["a"][:], in1=tmp["b"][:], op=ALU.min)
+            else:
+                nc.vector.quantize_mx(out=bc[:, k, :].bitcast(FP8X4), scales=bsc[:, k, :], in_=tmp["g", k][:])
+
+        pieces = [("a", 0, 0.9)]
+        for k in range(1, 8):
+            pieces.extend([("a", k, 0.9), ("b", k, 0.9), ("m", k, 1.75), ("q", k - 1, 0.9)])
+        pieces.extend([("a", 8, 0.9), ("q", 7, 0.9), ("q", 8, 0.9)])
+
+        tpw = {}
+        grp = {}
+        wc = {}
+        ws = {}
+        acc = {}
+        ot = {}
+        tpo = {}
+
+        def w_transposes(j):
+            t, r = divmod(j, NR)
+            words = wn[t][:].bitcast(F32)
+            tpw[j] = bank("tpw")
+            for u in range(4):
+                first = 9 * u + r
+                nc.tensor.transpose(tpw[j][:, P * u:P * u + P], words[:, first:first + 36 * 127 + 1:36], ident_f[:])
+
+        def w_evac(j, on_vector):
+            grp[j] = gpool.tile([P, 1024], BF16, tag="grp", name="grp", align_bytes=64)
+            src = tpw[j][:].bitcast(BF16).rearrange("p (u o e) -> p e o u", u=4, o=P, e=2)
+            dst = grp[j][:].rearrange("p (e o u) -> p e o u", e=2, o=P, u=4)
+            if on_vector:
+                nc.vector.tensor_copy(out=dst, in_=src)
+            else:
+                nc.scalar.copy(out=dst, in_=src)
+
+        def w_quant(j):
+            t, r = divmod(j, NR)
+            if r == 0:
+                wc[t] = cpool.tile([P, 18, P], U32, tag="wc", name="wc", align_bytes=64)
+                ws[t] = cpool.tile([P, 18, P], U8, tag="ws", name="ws", align_bytes=64)
+            nc.vector.quantize_mx(out=wc[t][:, 2 * r:2 * r + 2, :].rearrange("p c o -> p (c o)").bitcast(FP8X4),
+                                  scales=ws[t][:, 2 * r:2 * r + 2, :].rearrange("p c o -> p (c o)"), in_=grp[j][:])
+
+        npass = [0] * NT
+
+        def mx_pass(t, idx):
+            if npass[t] == 0:
+                acc[t] = psum.tile([P, 512], F32, tag="acc", bufs=NA, name="acc")
+            first = npass[t] == 0
+            last = npass[t] == 19
+            if idx < 18:
+                h, k = divmod(idx, 9)
+                nc.tensor.matmul_mx(out=acc[t][:], lhsT=wc[t][:, idx, :].bitcast(FP8X4), lhsT_scale=ws[t][:, idx, :],
+                                    rhs=bc[:, k, 512 * h:512 * h + 512].bitcast(FP8X4),
+                                    rhs_scale=bsc[:, k, 512 * h:512 * h + 512], start=first, stop=last)
+            else:
+                g = idx - 18
+                nc.tensor.matmul_mx(out=acc[t][:], lhsT=bw[:, g, 256 * t:256 * t + 256].bitcast(FP4X4),
+                                    lhsT_scale=bs[:, g, P * t:P * t + P],
+                                    rhs=scod[:, 512 * g:512 * g + 512].bitcast(FP8X4),
+                                    rhs_scale=ssc[:, 512 * g:512 * g + 512], start=first, stop=last)
+            npass[t] += 1
+
+        def out1(t):
+            ot[t] = opool.tile([P, 512], F32, tag="ot", name="ot")
+            nc.scalar.activation(out=ot[t][:], in_=acc[t][:], func=AF.Identity, bias=bcol[:, t:t + 1], scale=1.0)
+
+        def out2(t):
+            tpo[t] = bank("tpo")
+            for bt in range(4):
+                nc.tensor.transpose(tpo[t][:, P * bt:P * bt + P], ot[t][:, P * bt:P * bt + P], ident_f[:])
+
+        def out3(t):
+            ob = opool.tile([P, 4, P], F32, tag="ob", name="ob")
+            nc.vector.tensor_copy(out=ob[:].rearrange("p t o -> p (t o)"), in_=tpo[t][:])
+            nc.sync.dma_start(out=out.rearrange("(t p) o -> p t o", p=P)[:, :, P * t:P * t + P], in_=ob[:])
+
+        BIG = 10 ** 6
+        wq_step = [[BIG] * 20 for t in range(NT)]
+        for t in range(NT):
+            wq_step[t][18] = -1
+            wq_step[t][19] = -1
+        kb_step = [BIG] * 9
+        sent = [[False] * 20 for t in range(NT)]
+        done_step = [BIG] * NT
+        o1_step = [BIG] * NT
+        o2_step = [BIG] * NT
+        o3_step = [BIG] * NT
+        nbank = 0
+        nquant = 0
+        npiece = 0
+        credit = 0.0
+        step = 0
+        while min(1 if o3_step[t] < BIG else 0 for t in range(NT)) == 0:
+            assert step < 500
+            for t in range(NT):
+                if o1_step[t] < step and o2_step[t] == BIG:
+                    out2(t)
+                    o2_step[t] = step
+            new = []
+            for i in range(GB):
+                if nbank < NT * NR:
+                    t, r = divmod(nbank, NR)
+                    if r > 0 or t < NW or done_step[t - NW] < BIG:
+                        w_transposes(nbank)
+                        new.append(nbank)
+                        nbank += 1
+                        if r == NR - 1 and t + 2 < NT:
+                            load_w(t + 2)
+            for t in range(NT):
+                if done_step[t] < step and o1_step[t] == BIG:
+                    out1(t)
+                    o1_step[t] = step
+            for j in new:
+                w_evac(j, npiece >= len(pieces) and j % 3 == 2)
+            for t in range(NT):
+                if o2_step[t] <= step and o3_step[t] == BIG:
+                    out3(t)
+                    o3_step[t] = step
+            while nquant < nbank - len(new):
+                t, r = divmod(nquant, NR)
+                w_quant(nquant)
+                wq_step[t][2 * r] = step
+                wq_step[t][2 * r + 1] = step
+                nquant += 1
+            credit = min(credit, 0.0) + (BQ if len(new) == GB else 2 * BQ)
+            while npiece < len(pieces) and credit > 0:
+                kind, k, cost = pieces[npiece]
+                piece(kind, k)
+                if kind == "q":
+                    kb_step[k] = step
+                credit -= cost
+                npiece += 1
+            for t in range(NT):
+                if t >= NA and o1_step[t - NA] == BIG:
+                    continue
+                for idx in [18, 19] + list(range(18)):
+                    if sent[t][idx] or wq_step[t][idx] >= step:
+                        continue
+                    if idx < 18 and kb_step[idx % 9] >= step:
+                        continue
+                    mx_pass(t, idx)
+                    sent[t][idx] = True
+                    if npass[t] == 20:
+                        done_step[t] = step
+            step += 1

@@ -19,12 +19,17 @@ P = 128
 NT = 8
 NR = 9
 MANUAL = False
-NA = 4
+NA = 5
 NTP = 8 - NA
 NW = 5
 GB = 3
 BQ = 2
-NG = 8
+NG = 6
+ESH = 3
+MXC = 10
+DSET = (5, 6, 7)
+NWN = 3
+DSH = 2
 
 
 def tile_kanbasislinear_kernel(tc, x, spline_weight, base_weight_words, base_weight_scales, bias, out):
@@ -32,7 +37,7 @@ def tile_kanbasislinear_kernel(tc, x, spline_weight, base_weight_words, base_wei
     with ExitStack() as ctx:
         const = ctx.enter_context(tc.tile_pool(name="const", bufs=1))
         work = ctx.enter_context(tc.tile_pool(name="work", bufs=1))
-        wnat = ctx.enter_context(tc.tile_pool(name="wnat", bufs=2))
+        wnat = ctx.enter_context(tc.tile_pool(name="wnat", bufs=NWN))
         gpool = ctx.enter_context(tc.tile_pool(name="gpool", bufs=NG))
         cpool = ctx.enter_context(tc.tile_pool(name="cpool", bufs=NW))
         opool = ctx.enter_context(tc.tile_pool(name="opool", bufs=2))
@@ -46,7 +51,7 @@ def tile_kanbasislinear_kernel(tc, x, spline_weight, base_weight_words, base_wei
         warm = const.tile([P, 2], F32, name="warm")
         nc.vector.memset(warm[:], 0.0)
         nc.scalar.activation(out=warm[:, 1:2], in_=warm[:, 0:1], func=AF.Silu)
-        x_sb = work.tile([P, 4, 1024], BF16, tag="bg", bufs=2, name="x_sb", align_bytes=64)
+        x_sb = wnat.tile([P, 4, 1024], BF16, tag="wn", name="x_sb")
         nc.sync.dma_start(out=x_sb[:], in_=x.rearrange("(t p) i -> p t i", p=P))
         ident_f = const.tile([P, P], F32, name="ident_f")
         make_identity(nc, ident_f[:])
@@ -61,8 +66,13 @@ def tile_kanbasislinear_kernel(tc, x, spline_weight, base_weight_words, base_wei
         wn = {}
 
         def load_w(t):
-            wn[t] = wnat.tile([P, 9216], BF16, tag="wn", name="wn")
-            nc.sync.dma_start(out=wn[t][:], in_=spline_weight[P * t:P * t + P].rearrange("o i k -> o (i k)"))
+            rows = spline_weight[P * t:P * t + P]
+            if t in DSET:
+                wn[t] = wnat.tile([P, P, 80], BF16, tag="wn", name="wd")
+                nc.sync.dma_start(out=wn[t][:, :, 0:72], in_=rows.rearrange("o (p a) k -> p o (a k)", p=P, a=8))
+            else:
+                wn[t] = wnat.tile([P, 9216], BF16, tag="wn", name="wn")
+                nc.sync.dma_start(out=wn[t][:], in_=rows.rearrange("o i k -> o (i k)"))
 
         load_w(0)
         nc.sync.dma_start(out=brow[0:8, :], in_=bias.rearrange("(t p) -> t p", p=P))
@@ -70,10 +80,11 @@ def tile_kanbasislinear_kernel(tc, x, spline_weight, base_weight_words, base_wei
         for r in range(4):
             nc.sync.dma_start(out=bs[r:P:32, :, :].bitcast(I32), in_=sc_rows[r:16:4].bitcast(I32))
         nc.sync.dma_start(out=bw[:].bitcast(I32), in_=base_weight_words.rearrange("g p n -> p g n").bitcast(I32))
-        load_w(1)
+        for t in range(1, NWN - 1):
+            load_w(t)
 
         xw = x_sb[:].bitcast(F32)
-        xp = work.tile([P, 2, 512, 4], BF16, tag="ra", name="xp")
+        xp = cpool.tile([P, 2, 512, 4], BF16, tag="wc", name="xp", align_bytes=64)
         for bt in range(4):
             tpx = bank("tpx")
             for u in range(4):
@@ -90,7 +101,7 @@ def tile_kanbasislinear_kernel(tc, x, spline_weight, base_weight_words, base_wei
                                 op0=ALU.max, op1=ALU.min)
         nc.vector.tensor_scalar(out=nxs[:], in0=xs[:], scalar1=-1.0, scalar2=None, op0=ALU.mult)
 
-        sg = work.tile([P, 2, 512, 4], BF16, tag="bg", bufs=2, name="sg", align_bytes=64)
+        sg = [work.tile([P, 512, 4], BF16, tag="bg", bufs=3, name="sg", align_bytes=64) for g in range(2)]
         for bt in range(4):
             tps = bank("tps")
             for g in range(2):
@@ -99,7 +110,7 @@ def tile_kanbasislinear_kernel(tc, x, spline_weight, base_weight_words, base_wei
                                         xw[:, bt, 256 * g + u:256 * (g + 1):2], ident_f[:])
             v = tps[:].bitcast(BF16).rearrange("p (g u b e) -> p g b u e", g=2, u=2, b=P, e=2)
             for g in range(2):
-                nc.scalar.activation(out=sg[:, g, P * bt:P * bt + P, :].rearrange("p b (u e) -> p b u e", u=2, e=2),
+                nc.scalar.activation(out=sg[g][:, P * bt:P * bt + P, :].rearrange("p b (u e) -> p b u e", u=2, e=2),
                                      in_=v[:, g], func=AF.Silu)
         tpb = psum.tile([P, P], BF16, tag="tp", bufs=NTP, name="tpb")
         nc.tensor.transpose(tpb[:], brow[:], ident_b[:])
@@ -107,40 +118,51 @@ def tile_kanbasislinear_kernel(tc, x, spline_weight, base_weight_words, base_wei
         nc.vector.tensor_copy(out=bcol[:], in_=tpb[:, 0:8])
         scod = const.tile([P, 1024], U32, name="scod", align_bytes=64)
         ssc = const.tile([P, 1024], U8, name="ssc", align_bytes=64)
-        nc.vector.quantize_mx(out=scod[:].bitcast(FP8X4), scales=ssc[:], in_=sg[:].rearrange("p g b t -> p (g b t)"))
+        for g in range(2):
+            nc.vector.quantize_mx(out=scod[:, 512 * g:512 * g + 512].bitcast(FP8X4), scales=ssc[:, 512 * g:512 * g + 512],
+                                  in_=sg[g][:].rearrange("p b t -> p (b t)"))
+        load_w(NWN - 1)
 
         bc = const.tile([P, 9, 1024], U32, name="bc", align_bytes=64)
         bsc = const.tile([P, 9, 1024], U8, name="bsc", align_bytes=64)
         tmp = {}
 
-        def new_bg(k):
-            tmp["g", k] = work.tile([P, 4096], BF16, tag="bg", bufs=2, name="bg", align_bytes=64)
-            return tmp["g", k]
+        def new_bg(c):
+            tmp["g", c] = work.tile([P, 2048], BF16, tag="bg", bufs=3, name="bg", align_bytes=64)
+            return tmp["g", c]
 
-        def ramp(dst, src, shift):
-            nc.vector.tensor_scalar(out=dst[:], in0=src[:], scalar1=float(shift), scalar2=0.0, op0=ALU.add, op1=ALU.max)
+        def ramp(dst, src, h, shift):
+            nc.vector.tensor_scalar(out=dst[:], in0=src[:, 2048 * h:2048 * h + 2048], scalar1=float(shift), scalar2=0.0,
+                                    op0=ALU.add, op1=ALU.max)
 
-        def piece(kind, k):
+        def piece(kind, c):
+            h, k = divmod(c, 9)
             if kind == "a":
                 if k == 0:
-                    ramp(new_bg(k), nxs, -3)
+                    ramp(new_bg(c), nxs, h, -3)
                 elif k == 8:
-                    ramp(new_bg(k), xs, -3)
+                    ramp(new_bg(c), xs, h, -3)
                 else:
-                    tmp["a"] = work.tile([P, 4096], BF16, tag="ra", name="ra")
-                    ramp(tmp["a"], xs, 5 - k)
+                    tmp["a"] = work.tile([P, 2048], BF16, tag="ra", name="ra")
+                    ramp(tmp["a"], xs, h, 5 - k)
             elif kind == "b":
-                tmp["b"] = work.tile([P, 4096], BF16, tag="rb", name="rb")
-                ramp(tmp["b"], nxs, k - 3)
+                tmp["b"] = work.tile([P, 2048], BF16, tag="rb", name="rb")
+                ramp(tmp["b"], nxs, h, k - 3)
             elif kind == "m":
-                nc.vector.tensor_tensor(out=new_bg(k)[:], in0=tmp["a"][:], in1=tmp["b"][:], op=ALU.min)
+                nc.vector.tensor_tensor(out=new_bg(c)[:], in0=tmp["a"][:], in1=tmp["b"][:], op=ALU.min)
             else:
-                nc.vector.quantize_mx(out=bc[:, k, :].bitcast(FP8X4), scales=bsc[:, k, :], in_=tmp["g", k][:])
+                nc.vector.quantize_mx(out=bc[:, k, 512 * h:512 * h + 512].bitcast(FP8X4),
+                                      scales=bsc[:, k, 512 * h:512 * h + 512], in_=tmp["g", c][:])
 
-        pieces = [("a", 0, 0.9)]
-        for k in range(1, 8):
-            pieces.extend([("a", k, 0.9), ("b", k, 0.9), ("m", k, 1.75), ("q", k - 1, 0.9)])
-        pieces.extend([("a", 8, 0.9), ("q", 7, 0.9), ("q", 8, 0.9)])
+        pieces = []
+        for c in range(18):
+            if c % 9 in (0, 8):
+                pieces.append(("a", c, 0.5))
+            else:
+                pieces.extend([("a", c, 0.5), ("b", c, 0.5), ("m", c, 0.9)])
+            if c > 0:
+                pieces.append(("q", c - 1, 0.46))
+        pieces.append(("q", 17, 0.46))
 
         tpw = {}
         grp = {}
@@ -152,6 +174,8 @@ def tile_kanbasislinear_kernel(tc, x, spline_weight, base_weight_words, base_wei
 
         def w_transposes(j):
             t, r = divmod(j, NR)
+            if t in DSET:
+                return
             words = wn[t][:].bitcast(F32)
             tpw[j] = bank("tpw")
             for u in range(4):
@@ -160,8 +184,13 @@ def tile_kanbasislinear_kernel(tc, x, spline_weight, base_weight_words, base_wei
 
         def w_evac(j, on_vector):
             grp[j] = gpool.tile([P, 1024], BF16, tag="grp", name="grp", align_bytes=64)
-            src = tpw[j][:].bitcast(BF16).rearrange("p (u o e) -> p e o u", u=4, o=P, e=2)
-            dst = grp[j][:].rearrange("p (e o u) -> p e o u", e=2, o=P, u=4)
+            t, r = divmod(j, NR)
+            if t in DSET:
+                src = wn[t][:, :, 0:72].rearrange("p o (u c) -> p o c u", u=4, c=18)[:, :, 2 * r:2 * r + 2, :]
+                dst = grp[j][:].rearrange("p (e o u) -> p o e u", e=2, o=P, u=4)
+            else:
+                src = tpw[j][:].bitcast(BF16).rearrange("p (u o e) -> p e o u", u=4, o=P, e=2)
+                dst = grp[j][:].rearrange("p (e o u) -> p e o u", e=2, o=P, u=4)
             if on_vector:
                 nc.vector.tensor_copy(out=dst, in_=src)
             else:
@@ -214,7 +243,7 @@ def tile_kanbasislinear_kernel(tc, x, spline_weight, base_weight_words, base_wei
         for t in range(NT):
             wq_step[t][18] = -1
             wq_step[t][19] = -1
-        kb_step = [BIG] * 9
+        kb_step = [BIG] * 18
         sent = [[False] * 20 for t in range(NT)]
         done_step = [BIG] * NT
         o1_step = [BIG] * NT
@@ -231,26 +260,29 @@ def tile_kanbasislinear_kernel(tc, x, spline_weight, base_weight_words, base_wei
                 if o1_step[t] < step and o2_step[t] == BIG:
                     out2(t)
                     o2_step[t] = step
+                    out3(t)
+                    o3_step[t] = step
+            n_o1 = 0
+            for t in range(NT):
+                if done_step[t] < step and o1_step[t] == BIG and n_o1 < 2:
+                    out1(t)
+                    o1_step[t] = step
+                    n_o1 += 1
             new = []
             for i in range(GB):
                 if nbank < NT * NR:
                     t, r = divmod(nbank, NR)
                     if r > 0 or t < NW or done_step[t - NW] < BIG:
-                        w_transposes(nbank)
-                        new.append(nbank)
+                        j = nbank
+                        w_transposes(j)
+                        if t in DSET:
+                            w_evac(j, DSH == 0 or j % DSH != 0)
+                        else:
+                            w_evac(j, npiece >= len(pieces) and j % ESH == 0)
+                        new.append(j)
                         nbank += 1
-                        if r == NR - 1 and t + 2 < NT:
-                            load_w(t + 2)
-            for t in range(NT):
-                if done_step[t] < step and o1_step[t] == BIG:
-                    out1(t)
-                    o1_step[t] = step
-            for j in new:
-                w_evac(j, npiece >= len(pieces) and j % 3 == 2)
-            for t in range(NT):
-                if o2_step[t] <= step and o3_step[t] == BIG:
-                    out3(t)
-                    o3_step[t] = step
+                        if r == NR - 1 and t + NWN < NT:
+                            load_w(t + NWN)
             while nquant < nbank - len(new):
                 t, r = divmod(nquant, NR)
                 w_quant(nquant)
@@ -265,15 +297,17 @@ def tile_kanbasislinear_kernel(tc, x, spline_weight, base_weight_words, base_wei
                     kb_step[k] = step
                 credit -= cost
                 npiece += 1
+            nmx = 0
             for t in range(NT):
                 if t >= NA and o1_step[t - NA] == BIG:
                     continue
                 for idx in [18, 19] + list(range(18)):
-                    if sent[t][idx] or wq_step[t][idx] >= step:
+                    if sent[t][idx] or wq_step[t][idx] >= step or nmx >= MXC:
                         continue
-                    if idx < 18 and kb_step[idx % 9] >= step:
+                    if idx < 18 and kb_step[idx] >= step:
                         continue
                     mx_pass(t, idx)
+                    nmx += 1
                     sent[t][idx] = True
                     if npass[t] == 20:
                         done_step[t] = step

@@ -236,7 +236,7 @@ def tile_kanbasislinear_kernel(tc, x, spline_weight, base_weight_words, base_wei
         def out3(t):
             ob = opool.tile([P, 4, P], F32, tag="ob", name="ob")
             nc.vector.tensor_copy(out=ob[:].rearrange("p t o -> p (t o)"), in_=tpo[t][:])
-            nc.sync.dma_start(out=out.rearrange("(t p) o -> p t o", p=P)[:, :, P * t:P * t + P], in_=ob[:])
+            nc.gpsimd.dma_start(out=out.rearrange("(t p) o -> p t o", p=P)[:, :, P * t:P * t + P], in_=ob[:])
 
         BIG = 10 ** 6
         wq_step = [[BIG] * 20 for t in range(NT)]

@@ -21,15 +21,18 @@ NR = 9
 MANUAL = False
 NA = 5
 NTP = 8 - NA
-NW = 5
+NW = 7
 GB = 3
 BQ = 2
 NG = 6
 ESH = 3
-MXC = 10
-DSET = (5, 6, 7)
-NWN = 3
-DSH = 2
+O3M = 4
+O3A = 2
+XA = 2
+MXC = 8
+DSET = ()
+NWN = 2
+DSH = 0
 
 
 def tile_kanbasislinear_kernel(tc, x, spline_weight, base_weight_words, base_weight_scales, bias, out):
@@ -46,7 +49,7 @@ def tile_kanbasislinear_kernel(tc, x, spline_weight, base_weight_words, base_wei
             ctx.enter_context(tc.manual_schedule())
 
         def bank(name):
-            return psum.tile([P, 512], F32, tag="tp", bufs=NTP, name=name)
+            return psum.tile([P, 512], F32, tag="bk", bufs=8, name=name)
 
         warm = const.tile([P, 2], F32, name="warm")
         nc.vector.memset(warm[:], 0.0)
@@ -91,7 +94,7 @@ def tile_kanbasislinear_kernel(tc, x, spline_weight, base_weight_words, base_wei
                 nc.tensor.transpose(tpx[:, P * u:P * u + P], xw[:, bt, u:512:4], ident_f[:])
             src = tpx[:].bitcast(BF16).rearrange("p (u b e) -> p e b u", u=4, b=P, e=2)
             dst = xp[:, :, P * bt:P * bt + P, :]
-            if bt % 2 == 0:
+            if bt < XA:
                 nc.scalar.activation(out=dst, in_=src, func=AF.Copy, scale=2.0)
             else:
                 nc.vector.tensor_scalar(out=dst, in0=src, scalar1=2.0, scalar2=None, op0=ALU.mult)
@@ -112,7 +115,7 @@ def tile_kanbasislinear_kernel(tc, x, spline_weight, base_weight_words, base_wei
             for g in range(2):
                 nc.scalar.activation(out=sg[g][:, P * bt:P * bt + P, :].rearrange("p b (u e) -> p b u e", u=2, e=2),
                                      in_=v[:, g], func=AF.Silu)
-        tpb = psum.tile([P, P], BF16, tag="tp", bufs=NTP, name="tpb")
+        tpb = psum.tile([P, P], BF16, tag="bk", bufs=8, name="tpb")
         nc.tensor.transpose(tpb[:], brow[:], ident_b[:])
         bcol = const.tile([P, 8], F32, name="bcol")
         nc.vector.tensor_copy(out=bcol[:], in_=tpb[:, 0:8])
@@ -208,7 +211,7 @@ def tile_kanbasislinear_kernel(tc, x, spline_weight, base_weight_words, base_wei
 
         def mx_pass(t, idx):
             if npass[t] == 0:
-                acc[t] = psum.tile([P, 512], F32, tag="acc", bufs=NA, name="acc")
+                acc[t] = psum.tile([P, 512], F32, tag="bk", bufs=8, name="acc")
             first = npass[t] == 0
             last = npass[t] == 19
             if idx < 18:
@@ -235,8 +238,11 @@ def tile_kanbasislinear_kernel(tc, x, spline_weight, base_weight_words, base_wei
 
         def out3(t):
             ob = opool.tile([P, 4, P], F32, tag="ob", name="ob")
-            nc.vector.tensor_copy(out=ob[:].rearrange("p t o -> p (t o)"), in_=tpo[t][:])
-            nc.gpsimd.dma_start(out=out.rearrange("(t p) o -> p t o", p=P)[:, :, P * t:P * t + P], in_=ob[:])
+            if t % O3M < O3A:
+                nc.scalar.copy(out=ob[:].rearrange("p t o -> p (t o)"), in_=tpo[t][:])
+            else:
+                nc.vector.tensor_copy(out=ob[:].rearrange("p t o -> p (t o)"), in_=tpo[t][:])
+            nc.sync.dma_start(out=out.rearrange("(t p) o -> p t o", p=P)[:, :, P * t:P * t + P], in_=ob[:])
 
         BIG = 10 ** 6
         wq_step = [[BIG] * 20 for t in range(NT)]

@@ -18,7 +18,7 @@ FLOPS = 2 * 512 * 1024 * 1024 * 10
 P = 128
 NT = 8
 NR = 9
-MANUAL = False
+MANUAL = True
 NA = 5
 NTP = 8 - NA
 NW = 7
@@ -30,6 +30,7 @@ O3M = 4
 O3A = 2
 XA = 2
 MXC = 8
+MXMIN = 1
 DSET = ()
 NWN = 2
 DSH = 0
@@ -228,21 +229,19 @@ def tile_kanbasislinear_kernel(tc, x, spline_weight, base_weight_words, base_wei
             npass[t] += 1
 
         def out1(t):
-            ot[t] = opool.tile([P, 512], F32, tag="ot", name="ot")
+            ot[t] = opool.tile([P, 512], F32, tag="ot", name="ot", align_bytes=64)
             nc.scalar.activation(out=ot[t][:], in_=acc[t][:], func=AF.Identity, bias=bcol[:, t:t + 1], scale=1.0)
 
         def out2(t):
-            tpo[t] = bank("tpo")
-            for bt in range(4):
-                nc.tensor.transpose(tpo[t][:, P * bt:P * bt + P], ot[t][:, P * bt:P * bt + P], ident_f[:])
+            z = opool.tile([P, 512], F32, tag="z", name="z", align_bytes=64)
+            nc.vector.transpose(out=z[:], in_=ot[t][:])
+            tpo[t] = z
 
         def out3(t):
-            ob = opool.tile([P, 4, P], F32, tag="ob", name="ob")
-            if t % O3M < O3A:
-                nc.scalar.copy(out=ob[:].rearrange("p t o -> p (t o)"), in_=tpo[t][:])
-            else:
-                nc.vector.tensor_copy(out=ob[:].rearrange("p t o -> p (t o)"), in_=tpo[t][:])
-            nc.sync.dma_start(out=out.rearrange("(t p) o -> p t o", p=P)[:, :, P * t:P * t + P], in_=ob[:])
+            rows = out.rearrange("(c w) o -> w c o", w=32)
+            for a in range(4):
+                nc.sync.dma_start(out=rows[:, :, P * t + 32 * a:P * t + 32 * a + 32],
+                                  in_=tpo[t][32 * a:32 * a + 32, :].rearrange("w (c r) -> w c r", r=32))
 
         BIG = 10 ** 6
         wq_step = [[BIG] * 20 for t in range(NT)]
@@ -303,17 +302,19 @@ def tile_kanbasislinear_kernel(tc, x, spline_weight, base_weight_words, base_wei
                     kb_step[k] = step
                 credit -= cost
                 npiece += 1
-            nmx = 0
+            ready = []
             for t in range(NT):
                 if t >= NA and o1_step[t - NA] == BIG:
                     continue
                 for idx in [18, 19] + list(range(18)):
-                    if sent[t][idx] or wq_step[t][idx] >= step or nmx >= MXC:
+                    if sent[t][idx] or wq_step[t][idx] >= step:
                         continue
                     if idx < 18 and kb_step[idx] >= step:
                         continue
+                    ready.append((t, idx))
+            if len(ready) >= MXMIN or nbank == NT * NR:
+                for t, idx in ready[:MXC]:
                     mx_pass(t, idx)
-                    nmx += 1
                     sent[t][idx] = True
                     if npass[t] == 20:
                         done_step[t] = step

@@ -18,7 +18,7 @@ FLOPS = 2 * 512 * 1024 * 1024 * 10
 P = 128
 NT = 8
 NR = 9
-MANUAL = True
+MANUAL = False
 NA = 5
 NTP = 8 - NA
 NW = 7
@@ -31,6 +31,11 @@ O3A = 2
 XA = 2
 MXC = 8
 MXMIN = 1
+WARM = 6
+XD = 1
+JD = 18
+LEAN = 0
+SQAT = 0
 DSET = ()
 NWN = 2
 DSH = 0
@@ -49,14 +54,29 @@ def tile_kanbasislinear_kernel(tc, x, spline_weight, base_weight_words, base_wei
         if MANUAL:
             ctx.enter_context(tc.manual_schedule())
 
-        def bank(name):
-            return psum.tile([P, 512], F32, tag="bk", bufs=8, name=name)
+        dz = const.tile([P, 512], BF16, name="dz")
+        nc.vector.memset(dz[:], 0.0)
+
+        def dummy(tile_ap):
+            nc.tensor.matmul(out=tile_ap[:], lhsT=dz[:, 0:P], rhs=dz[:], start=True, stop=True)
+
+        def bank(name, filler=False):
+            b = psum.tile([P, 512], F32, tag="bk", bufs=8, name=name)
+            if filler:
+                dummy(b)
+            return b
+
+        if WARM > 0:
+            wb = bank("wb")
+            for i in range(WARM):
+                dummy(wb)
 
         warm = const.tile([P, 2], F32, name="warm")
         nc.vector.memset(warm[:], 0.0)
         nc.scalar.activation(out=warm[:, 1:2], in_=warm[:, 0:1], func=AF.Silu)
         x_sb = wnat.tile([P, 4, 1024], BF16, tag="wn", name="x_sb")
-        nc.sync.dma_start(out=x_sb[:], in_=x.rearrange("(t p) i -> p t i", p=P))
+        for bt in range(4):
+            nc.sync.dma_start(out=x_sb[:, bt, :], in_=x[P * bt:P * bt + P, :])
         ident_f = const.tile([P, P], F32, name="ident_f")
         make_identity(nc, ident_f[:])
         ident_b = const.tile([P, P], BF16, name="ident_b")
@@ -90,7 +110,7 @@ def tile_kanbasislinear_kernel(tc, x, spline_weight, base_weight_words, base_wei
         xw = x_sb[:].bitcast(F32)
         xp = cpool.tile([P, 2, 512, 4], BF16, tag="wc", name="xp", align_bytes=64)
         for bt in range(4):
-            tpx = bank("tpx")
+            tpx = bank("tpx", XD > 0)
             for u in range(4):
                 nc.tensor.transpose(tpx[:, P * u:P * u + P], xw[:, bt, u:512:4], ident_f[:])
             src = tpx[:].bitcast(BF16).rearrange("p (u b e) -> p e b u", u=4, b=P, e=2)
@@ -101,13 +121,18 @@ def tile_kanbasislinear_kernel(tc, x, spline_weight, base_weight_words, base_wei
                 nc.vector.tensor_scalar(out=dst, in0=src, scalar1=2.0, scalar2=None, op0=ALU.mult)
         xs = const.tile([P, 4096], BF16, name="xs")
         nxs = const.tile([P, 4096], BF16, name="nxs")
-        nc.vector.tensor_scalar(out=xs[:], in0=xp[:].rearrange("p h b u -> p (h b u)"), scalar1=-4.0, scalar2=4.0,
-                                op0=ALU.max, op1=ALU.min)
-        nc.vector.tensor_scalar(out=nxs[:], in0=xs[:], scalar1=-1.0, scalar2=None, op0=ALU.mult)
+
+        def clamp(h):
+            half = slice(2048 * h, 2048 * h + 2048)
+            nc.vector.tensor_scalar(out=xs[:, half], in0=xp[:, h].rearrange("p b u -> p (b u)"), scalar1=-4.0, scalar2=4.0,
+                                    op0=ALU.max, op1=ALU.min)
+            nc.vector.tensor_scalar(out=nxs[:, half], in0=xs[:, half], scalar1=-1.0, scalar2=None, op0=ALU.mult)
+
+        clamp(0)
 
         sg = [work.tile([P, 512, 4], BF16, tag="bg", bufs=3, name="sg", align_bytes=64) for g in range(2)]
         for bt in range(4):
-            tps = bank("tps")
+            tps = bank("tps", XD > 0)
             for g in range(2):
                 for u in range(2):
                     nc.tensor.transpose(tps[:, P * (2 * g + u):P * (2 * g + u) + P],
@@ -122,9 +147,6 @@ def tile_kanbasislinear_kernel(tc, x, spline_weight, base_weight_words, base_wei
         nc.vector.tensor_copy(out=bcol[:], in_=tpb[:, 0:8])
         scod = const.tile([P, 1024], U32, name="scod", align_bytes=64)
         ssc = const.tile([P, 1024], U8, name="ssc", align_bytes=64)
-        for g in range(2):
-            nc.vector.quantize_mx(out=scod[:, 512 * g:512 * g + 512].bitcast(FP8X4), scales=ssc[:, 512 * g:512 * g + 512],
-                                  in_=sg[g][:].rearrange("p b t -> p (b t)"))
         load_w(NWN - 1)
 
         bc = const.tile([P, 9, 1024], U32, name="bc", align_bytes=64)
@@ -141,7 +163,12 @@ def tile_kanbasislinear_kernel(tc, x, spline_weight, base_weight_words, base_wei
 
         def piece(kind, c):
             h, k = divmod(c, 9)
-            if kind == "a":
+            if kind == "cl":
+                clamp(c)
+            elif kind == "sq":
+                nc.vector.quantize_mx(out=scod[:, 512 * c:512 * c + 512].bitcast(FP8X4), scales=ssc[:, 512 * c:512 * c + 512],
+                                      in_=sg[c][:].rearrange("p b t -> p (b t)"))
+            elif kind == "a":
                 if k == 0:
                     ramp(new_bg(c), nxs, h, -3)
                 elif k == 8:
@@ -166,6 +193,10 @@ def tile_kanbasislinear_kernel(tc, x, spline_weight, base_weight_words, base_wei
                 pieces.extend([("a", c, 0.5), ("b", c, 0.5), ("m", c, 0.9)])
             if c > 0:
                 pieces.append(("q", c - 1, 0.46))
+            if c == SQAT:
+                pieces.extend([("sq", 0, 0.46), ("sq", 1, 0.46)])
+            if c == 6:
+                pieces.append(("cl", 1, 1.0))
         pieces.append(("q", 17, 0.46))
 
         tpw = {}
@@ -181,7 +212,7 @@ def tile_kanbasislinear_kernel(tc, x, spline_weight, base_weight_words, base_wei
             if t in DSET:
                 return
             words = wn[t][:].bitcast(F32)
-            tpw[j] = bank("tpw")
+            tpw[j] = bank("tpw", j < JD or lean[0])
             for u in range(4):
                 first = 9 * u + r
                 nc.tensor.transpose(tpw[j][:, P * u:P * u + P], words[:, first:first + 36 * 127 + 1:36], ident_f[:])
@@ -209,6 +240,7 @@ def tile_kanbasislinear_kernel(tc, x, spline_weight, base_weight_words, base_wei
                                   scales=ws[t][:, 2 * r:2 * r + 2, :].rearrange("p c o -> p (c o)"), in_=grp[j][:])
 
         npass = [0] * NT
+        lean = [False]
 
         def mx_pass(t, idx):
             if npass[t] == 0:
@@ -245,9 +277,7 @@ def tile_kanbasislinear_kernel(tc, x, spline_weight, base_weight_words, base_wei
 
         BIG = 10 ** 6
         wq_step = [[BIG] * 20 for t in range(NT)]
-        for t in range(NT):
-            wq_step[t][18] = -1
-            wq_step[t][19] = -1
+        sq_step = [BIG, BIG]
         kb_step = [BIG] * 18
         sent = [[False] * 20 for t in range(NT)]
         done_step = [BIG] * NT
@@ -300,6 +330,9 @@ def tile_kanbasislinear_kernel(tc, x, spline_weight, base_weight_words, base_wei
                 piece(kind, k)
                 if kind == "q":
                     kb_step[k] = step
+                if kind == "sq":
+                    for t in range(NT):
+                        wq_step[t][18 + k] = step
                 credit -= cost
                 npiece += 1
             ready = []
@@ -312,6 +345,7 @@ def tile_kanbasislinear_kernel(tc, x, spline_weight, base_weight_words, base_wei
                     if idx < 18 and kb_step[idx] >= step:
                         continue
                     ready.append((t, idx))
+            lean[0] = LEAN > 0 and len(ready) < LEAN and nbank < NT * NR
             if len(ready) >= MXMIN or nbank == NT * NR:
                 for t, idx in ready[:MXC]:
                     mx_pass(t, idx)

@@ -16,29 +16,14 @@ AF = mybir.ActivationFunctionType
 FLOPS = 2 * 512 * 1024 * 1024 * 10
 
 P = 128
-NT = 8
-NR = 9
-MANUAL = False
-NA = 5
-NTP = 8 - NA
-NW = 7
-GB = 3
-BQ = 2
-NG = 6
-ESH = 3
-O3M = 4
-O3A = 2
-XA = 2
-MXC = 8
-MXMIN = 1
-WARM = 6
-XD = 1
-JD = 18
-LEAN = 0
-SQAT = 0
-DSET = ()
-NWN = 2
-DSH = 0
+TILES = 8
+BANKS = 9
+OPEN = 5
+CODES = 7
+STEP_BANKS = 3
+STEP_BASIS = 4
+STEP_PASSES = 8
+LATE = 10 ** 6
 
 
 def tile_kanbasislinear_kernel(tc, x, spline_weight, base_weight_words, base_weight_scales, bias, out):
@@ -46,30 +31,14 @@ def tile_kanbasislinear_kernel(tc, x, spline_weight, base_weight_words, base_wei
     with ExitStack() as ctx:
         const = ctx.enter_context(tc.tile_pool(name="const", bufs=1))
         work = ctx.enter_context(tc.tile_pool(name="work", bufs=1))
-        wnat = ctx.enter_context(tc.tile_pool(name="wnat", bufs=NWN))
-        gpool = ctx.enter_context(tc.tile_pool(name="gpool", bufs=NG))
-        cpool = ctx.enter_context(tc.tile_pool(name="cpool", bufs=NW))
+        wnat = ctx.enter_context(tc.tile_pool(name="wnat", bufs=2))
+        gpool = ctx.enter_context(tc.tile_pool(name="gpool", bufs=6))
+        cpool = ctx.enter_context(tc.tile_pool(name="cpool", bufs=CODES))
         opool = ctx.enter_context(tc.tile_pool(name="opool", bufs=2))
-        psum = ctx.enter_context(tc.psum_pool(name="psum", bufs=1))
-        if MANUAL:
-            ctx.enter_context(tc.manual_schedule())
+        psum = ctx.enter_context(tc.psum_pool(name="psum", bufs=8))
 
-        dz = const.tile([P, 512], BF16, name="dz")
-        nc.vector.memset(dz[:], 0.0)
-
-        def dummy(tile_ap):
-            nc.tensor.matmul(out=tile_ap[:], lhsT=dz[:, 0:P], rhs=dz[:], start=True, stop=True)
-
-        def bank(name, filler=False):
-            b = psum.tile([P, 512], F32, tag="bk", bufs=8, name=name)
-            if filler:
-                dummy(b)
-            return b
-
-        if WARM > 0:
-            wb = bank("wb")
-            for i in range(WARM):
-                dummy(wb)
+        def bank(name):
+            return psum.tile([P, 512], F32, tag="bank", name=name)
 
         warm = const.tile([P, 2], F32, name="warm")
         nc.vector.memset(warm[:], 0.0)
@@ -90,13 +59,9 @@ def tile_kanbasislinear_kernel(tc, x, spline_weight, base_weight_words, base_wei
         wn = {}
 
         def load_w(t):
-            rows = spline_weight[P * t:P * t + P]
-            if t in DSET:
-                wn[t] = wnat.tile([P, P, 80], BF16, tag="wn", name="wd")
-                nc.sync.dma_start(out=wn[t][:, :, 0:72], in_=rows.rearrange("o (p a) k -> p o (a k)", p=P, a=8))
-            else:
-                wn[t] = wnat.tile([P, 9216], BF16, tag="wn", name="wn")
-                nc.sync.dma_start(out=wn[t][:], in_=rows.rearrange("o i k -> o (i k)"))
+            wn[t] = wnat.tile([P, 4, 2304], BF16, tag="wn", name="wn")
+            quarters = spline_weight[P * t:P * t + P].rearrange("o (u m) k -> (o u) (m k)", u=4)
+            nc.sync.dma_start(out=wn[t][:], in_=quarters.rearrange("(g q) w -> q g w", q=P))
 
         load_w(0)
         nc.sync.dma_start(out=brow[0:8, :], in_=bias.rearrange("(t p) -> t p", p=P))
@@ -104,18 +69,16 @@ def tile_kanbasislinear_kernel(tc, x, spline_weight, base_weight_words, base_wei
         for r in range(4):
             nc.sync.dma_start(out=bs[r:P:32, :, :].bitcast(I32), in_=sc_rows[r:16:4].bitcast(I32))
         nc.sync.dma_start(out=bw[:].bitcast(I32), in_=base_weight_words.rearrange("g p n -> p g n").bitcast(I32))
-        for t in range(1, NWN - 1):
-            load_w(t)
 
         xw = x_sb[:].bitcast(F32)
         xp = cpool.tile([P, 2, 512, 4], BF16, tag="wc", name="xp", align_bytes=64)
         for bt in range(4):
-            tpx = bank("tpx", XD > 0)
+            tpx = bank("tpx")
             for u in range(4):
-                nc.tensor.transpose(tpx[:, P * u:P * u + P], xw[:, bt, u:512:4], ident_f[:])
+                nc.tensor.transpose(tpx[:, P * u:P * u + P], xw[:, bt, P * u:P * u + P], ident_f[:])
             src = tpx[:].bitcast(BF16).rearrange("p (u b e) -> p e b u", u=4, b=P, e=2)
             dst = xp[:, :, P * bt:P * bt + P, :]
-            if bt < XA:
+            if bt < 2:
                 nc.scalar.activation(out=dst, in_=src, func=AF.Copy, scale=2.0)
             else:
                 nc.vector.tensor_scalar(out=dst, in0=src, scalar1=2.0, scalar2=None, op0=ALU.mult)
@@ -132,7 +95,7 @@ def tile_kanbasislinear_kernel(tc, x, spline_weight, base_weight_words, base_wei
 
         sg = [work.tile([P, 512, 4], BF16, tag="bg", bufs=3, name="sg", align_bytes=64) for g in range(2)]
         for bt in range(4):
-            tps = bank("tps", XD > 0)
+            tps = bank("tps")
             for g in range(2):
                 for u in range(2):
                     nc.tensor.transpose(tps[:, P * (2 * g + u):P * (2 * g + u) + P],
@@ -141,16 +104,16 @@ def tile_kanbasislinear_kernel(tc, x, spline_weight, base_weight_words, base_wei
             for g in range(2):
                 nc.scalar.activation(out=sg[g][:, P * bt:P * bt + P, :].rearrange("p b (u e) -> p b u e", u=2, e=2),
                                      in_=v[:, g], func=AF.Silu)
-        tpb = psum.tile([P, P], BF16, tag="bk", bufs=8, name="tpb")
+        tpb = psum.tile([P, P], BF16, tag="bank", name="tpb")
         nc.tensor.transpose(tpb[:], brow[:], ident_b[:])
         bcol = const.tile([P, 8], F32, name="bcol")
         nc.vector.tensor_copy(out=bcol[:], in_=tpb[:, 0:8])
         scod = const.tile([P, 1024], U32, name="scod", align_bytes=64)
         ssc = const.tile([P, 1024], U8, name="ssc", align_bytes=64)
-        load_w(NWN - 1)
+        load_w(1)
 
-        bc = const.tile([P, 9, 1024], U32, name="bc", align_bytes=64)
-        bsc = const.tile([P, 9, 1024], U8, name="bsc", align_bytes=64)
+        bc = const.tile([P, 18, 512], U32, name="bc", align_bytes=64)
+        bsc = const.tile([P, 18, 512], U8, name="bsc", align_bytes=64)
         tmp = {}
 
         def new_bg(c):
@@ -163,12 +126,12 @@ def tile_kanbasislinear_kernel(tc, x, spline_weight, base_weight_words, base_wei
 
         def piece(kind, c):
             h, k = divmod(c, 9)
-            if kind == "cl":
+            if kind == "clamp":
                 clamp(c)
-            elif kind == "sq":
+            elif kind == "silu":
                 nc.vector.quantize_mx(out=scod[:, 512 * c:512 * c + 512].bitcast(FP8X4), scales=ssc[:, 512 * c:512 * c + 512],
                                       in_=sg[c][:].rearrange("p b t -> p (b t)"))
-            elif kind == "a":
+            elif kind == "up":
                 if k == 0:
                     ramp(new_bg(c), nxs, h, -3)
                 elif k == 8:
@@ -176,82 +139,66 @@ def tile_kanbasislinear_kernel(tc, x, spline_weight, base_weight_words, base_wei
                 else:
                     tmp["a"] = work.tile([P, 2048], BF16, tag="ra", name="ra")
                     ramp(tmp["a"], xs, h, 5 - k)
-            elif kind == "b":
+            elif kind == "down":
                 tmp["b"] = work.tile([P, 2048], BF16, tag="rb", name="rb")
                 ramp(tmp["b"], nxs, h, k - 3)
-            elif kind == "m":
+            elif kind == "min":
                 nc.vector.tensor_tensor(out=new_bg(c)[:], in0=tmp["a"][:], in1=tmp["b"][:], op=ALU.min)
             else:
-                nc.vector.quantize_mx(out=bc[:, k, 512 * h:512 * h + 512].bitcast(FP8X4),
-                                      scales=bsc[:, k, 512 * h:512 * h + 512], in_=tmp["g", c][:])
+                nc.vector.quantize_mx(out=bc[:, c, :].bitcast(FP8X4), scales=bsc[:, c, :], in_=tmp["g", c][:])
 
         pieces = []
         for c in range(18):
             if c % 9 in (0, 8):
-                pieces.append(("a", c, 0.5))
+                pieces.append(("up", c))
             else:
-                pieces.extend([("a", c, 0.5), ("b", c, 0.5), ("m", c, 0.9)])
+                pieces.extend([("up", c), ("down", c), ("min", c)])
             if c > 0:
-                pieces.append(("q", c - 1, 0.46))
-            if c == SQAT:
-                pieces.extend([("sq", 0, 0.46), ("sq", 1, 0.46)])
+                pieces.append(("quant", c - 1))
+            if c == 0:
+                pieces.extend([("silu", 0), ("silu", 1)])
             if c == 6:
-                pieces.append(("cl", 1, 1.0))
-        pieces.append(("q", 17, 0.46))
+                pieces.append(("clamp", 1))
+        pieces.append(("quant", 17))
 
-        tpw = {}
         grp = {}
         wc = {}
         ws = {}
         acc = {}
         ot = {}
-        tpo = {}
 
-        def w_transposes(j):
-            t, r = divmod(j, NR)
-            if t in DSET:
-                return
-            words = wn[t][:].bitcast(F32)
-            tpw[j] = bank("tpw", j < JD or lean[0])
-            for u in range(4):
-                first = 9 * u + r
-                nc.tensor.transpose(tpw[j][:, P * u:P * u + P], words[:, first:first + 36 * 127 + 1:36], ident_f[:])
-
-        def w_evac(j, on_vector):
+        def w_bank(j, on_vector):
+            t, r = divmod(j, BANKS)
+            tpw = bank("tpw")
+            for g in range(4):
+                words = wn[t][:, g, :].bitcast(F32)
+                nc.tensor.transpose(tpw[:, P * g:P * g + P], words[:, r:r + 9 * 127 + 1:9], ident_f[:])
             grp[j] = gpool.tile([P, 1024], BF16, tag="grp", name="grp", align_bytes=64)
-            t, r = divmod(j, NR)
-            if t in DSET:
-                src = wn[t][:, :, 0:72].rearrange("p o (u c) -> p o c u", u=4, c=18)[:, :, 2 * r:2 * r + 2, :]
-                dst = grp[j][:].rearrange("p (e o u) -> p o e u", e=2, o=P, u=4)
-            else:
-                src = tpw[j][:].bitcast(BF16).rearrange("p (u o e) -> p e o u", u=4, o=P, e=2)
-                dst = grp[j][:].rearrange("p (e o u) -> p e o u", e=2, o=P, u=4)
+            src = tpw[:].bitcast(BF16).rearrange("p (n e) -> p e n", e=2)
+            dst = grp[j][:].rearrange("p (e n) -> p e n", e=2)
             if on_vector:
                 nc.vector.tensor_copy(out=dst, in_=src)
             else:
                 nc.scalar.copy(out=dst, in_=src)
 
         def w_quant(j):
-            t, r = divmod(j, NR)
+            t, r = divmod(j, BANKS)
             if r == 0:
                 wc[t] = cpool.tile([P, 18, P], U32, tag="wc", name="wc", align_bytes=64)
                 ws[t] = cpool.tile([P, 18, P], U8, tag="ws", name="ws", align_bytes=64)
             nc.vector.quantize_mx(out=wc[t][:, 2 * r:2 * r + 2, :].rearrange("p c o -> p (c o)").bitcast(FP8X4),
                                   scales=ws[t][:, 2 * r:2 * r + 2, :].rearrange("p c o -> p (c o)"), in_=grp[j][:])
 
-        npass = [0] * NT
-        lean = [False]
+        npass = [0] * TILES
 
         def mx_pass(t, idx):
             if npass[t] == 0:
-                acc[t] = psum.tile([P, 512], F32, tag="bk", bufs=8, name="acc")
+                acc[t] = bank("acc")
             first = npass[t] == 0
             last = npass[t] == 19
             if idx < 18:
-                h, k = divmod(idx, 9)
                 nc.tensor.matmul_mx(out=acc[t][:], lhsT=wc[t][:, idx, :].bitcast(FP8X4), lhsT_scale=ws[t][:, idx, :],
-                                    rhs=bc[:, k, 512 * h:512 * h + 512].bitcast(FP8X4),
-                                    rhs_scale=bsc[:, k, 512 * h:512 * h + 512], start=first, stop=last)
+                                    rhs=bc[:, idx, :].bitcast(FP8X4), rhs_scale=bsc[:, idx, :], start=first, stop=last)
             else:
                 g = idx - 18
                 nc.tensor.matmul_mx(out=acc[t][:], lhsT=bw[:, g, 256 * t:256 * t + 256].bitcast(FP4X4),
@@ -260,96 +207,68 @@ def tile_kanbasislinear_kernel(tc, x, spline_weight, base_weight_words, base_wei
                                     rhs_scale=ssc[:, 512 * g:512 * g + 512], start=first, stop=last)
             npass[t] += 1
 
-        def out1(t):
+        def add_bias(t):
             ot[t] = opool.tile([P, 512], F32, tag="ot", name="ot", align_bytes=64)
             nc.scalar.activation(out=ot[t][:], in_=acc[t][:], func=AF.Identity, bias=bcol[:, t:t + 1], scale=1.0)
 
-        def out2(t):
+        def turn_and_store(t):
             z = opool.tile([P, 512], F32, tag="z", name="z", align_bytes=64)
             nc.vector.transpose(out=z[:], in_=ot[t][:])
-            tpo[t] = z
-
-        def out3(t):
             rows = out.rearrange("(c w) o -> w c o", w=32)
             for a in range(4):
                 nc.sync.dma_start(out=rows[:, :, P * t + 32 * a:P * t + 32 * a + 32],
-                                  in_=tpo[t][32 * a:32 * a + 32, :].rearrange("w (c r) -> w c r", r=32))
+                                  in_=z[32 * a:32 * a + 32, :].rearrange("w (c r) -> w c r", r=32))
 
-        BIG = 10 ** 6
-        wq_step = [[BIG] * 20 for t in range(NT)]
-        sq_step = [BIG, BIG]
-        kb_step = [BIG] * 18
-        sent = [[False] * 20 for t in range(NT)]
-        done_step = [BIG] * NT
-        o1_step = [BIG] * NT
-        o2_step = [BIG] * NT
-        o3_step = [BIG] * NT
+        w_step = [[LATE] * 20 for t in range(TILES)]
+        b_step = [LATE] * 18
+        sent = [[False] * 20 for t in range(TILES)]
+        done_step = [LATE] * TILES
+        bias_step = [LATE] * TILES
+        stored = [False] * TILES
         nbank = 0
         nquant = 0
         npiece = 0
-        credit = 0.0
         step = 0
-        while min(1 if o3_step[t] < BIG else 0 for t in range(NT)) == 0:
+        while not all(stored):
             assert step < 500
-            for t in range(NT):
-                if o1_step[t] < step and o2_step[t] == BIG:
-                    out2(t)
-                    o2_step[t] = step
-                    out3(t)
-                    o3_step[t] = step
-            n_o1 = 0
-            for t in range(NT):
-                if done_step[t] < step and o1_step[t] == BIG and n_o1 < 2:
-                    out1(t)
-                    o1_step[t] = step
-                    n_o1 += 1
-            new = []
-            for i in range(GB):
-                if nbank < NT * NR:
-                    t, r = divmod(nbank, NR)
-                    if r > 0 or t < NW or done_step[t - NW] < BIG:
-                        j = nbank
-                        w_transposes(j)
-                        if t in DSET:
-                            w_evac(j, DSH == 0 or j % DSH != 0)
-                        else:
-                            w_evac(j, npiece >= len(pieces) and j % ESH == 0)
-                        new.append(j)
-                        nbank += 1
-                        if r == NR - 1 and t + NWN < NT:
-                            load_w(t + NWN)
-            while nquant < nbank - len(new):
-                t, r = divmod(nquant, NR)
+            for t in range(TILES):
+                if bias_step[t] < step and not stored[t]:
+                    turn_and_store(t)
+                    stored[t] = True
+            for t in [t for t in range(TILES) if done_step[t] < step and bias_step[t] == LATE][:2]:
+                add_bias(t)
+                bias_step[t] = step
+            before = nbank
+            for i in range(STEP_BANKS):
+                t, r = divmod(nbank, BANKS)
+                if nbank < TILES * BANKS and (r > 0 or t < CODES or done_step[t - CODES] < LATE):
+                    w_bank(nbank, nbank % (3 if npiece >= len(pieces) else 1000) == 0)
+                    nbank += 1
+                    if r == BANKS - 1 and t + 2 < TILES:
+                        load_w(t + 2)
+            while nquant < before:
+                t, r = divmod(nquant, BANKS)
                 w_quant(nquant)
-                wq_step[t][2 * r] = step
-                wq_step[t][2 * r + 1] = step
+                w_step[t][2 * r] = step
+                w_step[t][2 * r + 1] = step
                 nquant += 1
-            credit = min(credit, 0.0) + (BQ if len(new) == GB else 2 * BQ)
-            while npiece < len(pieces) and credit > 0:
-                kind, k, cost = pieces[npiece]
-                piece(kind, k)
-                if kind == "q":
-                    kb_step[k] = step
-                if kind == "sq":
-                    for t in range(NT):
-                        wq_step[t][18 + k] = step
-                credit -= cost
+            for kind, c in pieces[npiece:npiece + (STEP_BASIS if nbank - before == STEP_BANKS else 2 * STEP_BASIS)]:
+                piece(kind, c)
+                if kind == "quant":
+                    b_step[c] = step
+                if kind == "silu":
+                    for t in range(TILES):
+                        w_step[t][18 + c] = step
                 npiece += 1
             ready = []
-            for t in range(NT):
-                if t >= NA and o1_step[t - NA] == BIG:
-                    continue
-                for idx in [18, 19] + list(range(18)):
-                    if sent[t][idx] or wq_step[t][idx] >= step:
-                        continue
-                    if idx < 18 and kb_step[idx] >= step:
-                        continue
-                    ready.append((t, idx))
-            lean[0] = LEAN > 0 and len(ready) < LEAN and nbank < NT * NR
-            if len(ready) >= MXMIN or nbank == NT * NR:
-                for t, idx in ready[:MXC]:
-                    mx_pass(t, idx)
-                    sent[t][idx] = True
-                    if npass[t] == 20:
-                        done_step[t] = step
+            for t in range(TILES):
+                if t < OPEN or bias_step[t - OPEN] < LATE:
+                    for idx in [18, 19] + list(range(18)):
+                        if not sent[t][idx] and w_step[t][idx] < step and (idx >= 18 or b_step[idx] < step):
+                            ready.append((t, idx))
+            for t, idx in ready[:STEP_PASSES]:
+                mx_pass(t, idx)
+                sent[t][idx] = True
+                if npass[t] == 20:
+                    done_step[t] = step
             step += 1

@@ -18,12 +18,13 @@ FLOPS = 2 * 512 * 1024 * 1024 * 10
 P = 128
 TILES = 8
 BANKS = 9
+PASSES = 20
 OPEN = 5
-CODES = 7
+CODES = 6
 STEP_BANKS = 3
 STEP_BASIS = 4
 STEP_PASSES = 8
-LATE = 10 ** 6
+NEVER = 10 ** 6
 
 
 def tile_kanbasislinear_kernel(tc, x, spline_weight, base_weight_words, base_weight_scales, bias, out):
@@ -32,7 +33,7 @@ def tile_kanbasislinear_kernel(tc, x, spline_weight, base_weight_words, base_wei
         const = ctx.enter_context(tc.tile_pool(name="const", bufs=1))
         work = ctx.enter_context(tc.tile_pool(name="work", bufs=1))
         wnat = ctx.enter_context(tc.tile_pool(name="wnat", bufs=2))
-        gpool = ctx.enter_context(tc.tile_pool(name="gpool", bufs=6))
+        gpool = ctx.enter_context(tc.tile_pool(name="gpool", bufs=8))
         cpool = ctx.enter_context(tc.tile_pool(name="cpool", bufs=CODES))
         opool = ctx.enter_context(tc.tile_pool(name="opool", bufs=2))
         psum = ctx.enter_context(tc.psum_pool(name="psum", bufs=8))
@@ -50,225 +51,229 @@ def tile_kanbasislinear_kernel(tc, x, spline_weight, base_weight_words, base_wei
         make_identity(nc, ident_f[:])
         ident_b = const.tile([P, P], BF16, name="ident_b")
         make_identity(nc, ident_b[:])
-        brow = const.tile([P, P], BF16, name="brow")
-        nc.vector.memset(brow[:], 0.0)
-        bs = const.tile([P, 2, 1024], U8, name="bs", align_bytes=64)
-        nc.vector.memset(bs[:].bitcast(I32), 0)
-        bw = const.tile([P, 2, 2048], U8, name="bw", align_bytes=64)
+        bias_rows = const.tile([P, P], BF16, name="brow")
+        nc.vector.memset(bias_rows[:], 0.0)
+        base_scales = const.tile([P, 2, 1024], U8, name="bs", align_bytes=64)
+        nc.vector.memset(base_scales[:].bitcast(I32), 0)
+        base_words = const.tile([P, 2, 2048], U8, name="bw", align_bytes=64)
+        nc.sync.dma_start(out=bias_rows[0:8, :], in_=bias.rearrange("(t p) -> t p", p=P))
+        raw = {}
 
-        wn = {}
-
-        def load_w(t):
-            wn[t] = wnat.tile([P, 4, 2304], BF16, tag="wn", name="wn")
+        def load_weights(t):
+            raw[t] = wnat.tile([P, 4, 2304], BF16, tag="wn", name="wn")
             quarters = spline_weight[P * t:P * t + P].rearrange("o (u m) k -> (o u) (m k)", u=4)
-            nc.sync.dma_start(out=wn[t][:], in_=quarters.rearrange("(g q) w -> q g w", q=P))
+            nc.sync.dma_start(out=raw[t][:], in_=quarters.rearrange("(g q) w -> q g w", q=P))
 
-        load_w(0)
-        nc.sync.dma_start(out=brow[0:8, :], in_=bias.rearrange("(t p) -> t p", p=P))
-        sc_rows = base_weight_scales.rearrange("g q n -> q g n")
+        load_weights(0)
+        scale_rows = base_weight_scales.rearrange("g q n -> q g n")
         for r in range(4):
-            nc.sync.dma_start(out=bs[r:P:32, :, :].bitcast(I32), in_=sc_rows[r:16:4].bitcast(I32))
-        nc.sync.dma_start(out=bw[:].bitcast(I32), in_=base_weight_words.rearrange("g p n -> p g n").bitcast(I32))
+            nc.sync.dma_start(out=base_scales[r:P:32, :, :].bitcast(I32), in_=scale_rows[r:16:4].bitcast(I32))
+        nc.sync.dma_start(out=base_words[:].bitcast(I32), in_=base_weight_words.rearrange("g p n -> p g n").bitcast(I32))
 
-        xw = x_sb[:].bitcast(F32)
-        xp = cpool.tile([P, 2, 512, 4], BF16, tag="wc", name="xp", align_bytes=64)
+        x_words = x_sb[:].bitcast(F32)
+        twice_x = cpool.tile([P, 2, 512, 4], BF16, tag="wc", name="xp", align_bytes=64)
         for bt in range(4):
-            tpx = bank("tpx")
+            turned = bank("tpx")
             for u in range(4):
-                nc.tensor.transpose(tpx[:, P * u:P * u + P], xw[:, bt, P * u:P * u + P], ident_f[:])
-            src = tpx[:].bitcast(BF16).rearrange("p (u b e) -> p e b u", u=4, b=P, e=2)
-            dst = xp[:, :, P * bt:P * bt + P, :]
+                nc.tensor.transpose(turned[:, P * u:P * u + P], x_words[:, bt, P * u:P * u + P], ident_f[:])
+            src = turned[:].bitcast(BF16).rearrange("p (u b e) -> p e b u", u=4, b=P, e=2)
+            dst = twice_x[:, :, P * bt:P * bt + P, :]
             if bt < 2:
                 nc.scalar.activation(out=dst, in_=src, func=AF.Copy, scale=2.0)
             else:
                 nc.vector.tensor_scalar(out=dst, in0=src, scalar1=2.0, scalar2=None, op0=ALU.mult)
-        xs = const.tile([P, 4096], BF16, name="xs")
-        nxs = const.tile([P, 4096], BF16, name="nxs")
+        pos = const.tile([P, 4096], BF16, name="xs")
+        neg = const.tile([P, 4096], BF16, name="nxs")
 
-        def clamp(h):
+        def clip(h):
             half = slice(2048 * h, 2048 * h + 2048)
-            nc.vector.tensor_scalar(out=xs[:, half], in0=xp[:, h].rearrange("p b u -> p (b u)"), scalar1=-4.0, scalar2=4.0,
-                                    op0=ALU.max, op1=ALU.min)
-            nc.vector.tensor_scalar(out=nxs[:, half], in0=xs[:, half], scalar1=-1.0, scalar2=None, op0=ALU.mult)
+            nc.vector.tensor_scalar(out=pos[:, half], in0=twice_x[:, h].rearrange("p b u -> p (b u)"), scalar1=-4.0,
+                                    scalar2=4.0, op0=ALU.max, op1=ALU.min)
+            nc.vector.tensor_scalar(out=neg[:, half], in0=pos[:, half], scalar1=-1.0, scalar2=None, op0=ALU.mult)
 
-        clamp(0)
+        clip(0)
 
-        sg = [work.tile([P, 512, 4], BF16, tag="bg", bufs=3, name="sg", align_bytes=64) for g in range(2)]
+        silu = [work.tile([P, 512, 4], BF16, tag="bg", bufs=3, name="sg", align_bytes=64) for g in range(2)]
         for bt in range(4):
-            tps = bank("tps")
+            turned = bank("tps")
             for g in range(2):
-                for u in range(2):
-                    nc.tensor.transpose(tps[:, P * (2 * g + u):P * (2 * g + u) + P],
-                                        xw[:, bt, 256 * g + u:256 * (g + 1):2], ident_f[:])
-            v = tps[:].bitcast(BF16).rearrange("p (g u b e) -> p g b u e", g=2, u=2, b=P, e=2)
+                for v in range(2):
+                    nc.tensor.transpose(turned[:, P * (2 * g + v):P * (2 * g + v) + P],
+                                        x_words[:, bt, 256 * g + v:256 * (g + 1):2], ident_f[:])
+            pairs = turned[:].bitcast(BF16).rearrange("p (g v b e) -> p g b v e", g=2, v=2, b=P, e=2)
             for g in range(2):
-                nc.scalar.activation(out=sg[g][:, P * bt:P * bt + P, :].rearrange("p b (u e) -> p b u e", u=2, e=2),
-                                     in_=v[:, g], func=AF.Silu)
-        tpb = psum.tile([P, P], BF16, tag="bank", name="tpb")
-        nc.tensor.transpose(tpb[:], brow[:], ident_b[:])
-        bcol = const.tile([P, 8], F32, name="bcol")
-        nc.vector.tensor_copy(out=bcol[:], in_=tpb[:, 0:8])
-        scod = const.tile([P, 1024], U32, name="scod", align_bytes=64)
-        ssc = const.tile([P, 1024], U8, name="ssc", align_bytes=64)
-        load_w(1)
+                nc.scalar.activation(out=silu[g][:, P * bt:P * bt + P, :].rearrange("p b (v e) -> p b v e", v=2, e=2),
+                                     in_=pairs[:, g], func=AF.Silu)
+        turned_bias = psum.tile([P, P], BF16, tag="bank", name="tpb")
+        nc.tensor.transpose(turned_bias[:], bias_rows[:], ident_b[:])
+        bias_col = const.tile([P, 8], F32, name="bcol")
+        nc.vector.tensor_copy(out=bias_col[:], in_=turned_bias[:, 0:8])
+        silu_codes = const.tile([P, 1024], U32, name="scod", align_bytes=64)
+        silu_scales = const.tile([P, 1024], U8, name="ssc", align_bytes=64)
+        load_weights(1)
 
-        bc = const.tile([P, 18, 512], U32, name="bc", align_bytes=64)
-        bsc = const.tile([P, 18, 512], U8, name="bsc", align_bytes=64)
-        tmp = {}
+        basis_codes = const.tile([P, 18, 512], U32, name="bc", align_bytes=64)
+        basis_scales = const.tile([P, 18, 512], U8, name="bsc", align_bytes=64)
+        live = {}
 
-        def new_bg(c):
-            tmp["g", c] = work.tile([P, 2048], BF16, tag="bg", bufs=3, name="bg", align_bytes=64)
-            return tmp["g", c]
+        def new_basis(c):
+            live["basis", c] = work.tile([P, 2048], BF16, tag="bg", bufs=3, name="bg", align_bytes=64)
+            return live["basis", c]
 
         def ramp(dst, src, h, shift):
             nc.vector.tensor_scalar(out=dst[:], in0=src[:, 2048 * h:2048 * h + 2048], scalar1=float(shift), scalar2=0.0,
                                     op0=ALU.add, op1=ALU.max)
 
-        def piece(kind, c):
+        def basis_instruction(kind, c):
             h, k = divmod(c, 9)
-            if kind == "clamp":
-                clamp(c)
+            if kind == "clip":
+                clip(c)
             elif kind == "silu":
-                nc.vector.quantize_mx(out=scod[:, 512 * c:512 * c + 512].bitcast(FP8X4), scales=ssc[:, 512 * c:512 * c + 512],
-                                      in_=sg[c][:].rearrange("p b t -> p (b t)"))
+                nc.vector.quantize_mx(out=silu_codes[:, 512 * c:512 * c + 512].bitcast(FP8X4),
+                                      scales=silu_scales[:, 512 * c:512 * c + 512],
+                                      in_=silu[c][:].rearrange("p b t -> p (b t)"))
             elif kind == "up":
                 if k == 0:
-                    ramp(new_bg(c), nxs, h, -3)
+                    ramp(new_basis(c), neg, h, -3)
                 elif k == 8:
-                    ramp(new_bg(c), xs, h, -3)
+                    ramp(new_basis(c), pos, h, -3)
                 else:
-                    tmp["a"] = work.tile([P, 2048], BF16, tag="ra", name="ra")
-                    ramp(tmp["a"], xs, h, 5 - k)
+                    live["up"] = work.tile([P, 2048], BF16, tag="ra", name="ra")
+                    ramp(live["up"], pos, h, 5 - k)
             elif kind == "down":
-                tmp["b"] = work.tile([P, 2048], BF16, tag="rb", name="rb")
-                ramp(tmp["b"], nxs, h, k - 3)
+                live["down"] = work.tile([P, 2048], BF16, tag="rb", name="rb")
+                ramp(live["down"], neg, h, k - 3)
             elif kind == "min":
-                nc.vector.tensor_tensor(out=new_bg(c)[:], in0=tmp["a"][:], in1=tmp["b"][:], op=ALU.min)
+                nc.vector.tensor_tensor(out=new_basis(c)[:], in0=live["up"][:], in1=live["down"][:], op=ALU.min)
             else:
-                nc.vector.quantize_mx(out=bc[:, c, :].bitcast(FP8X4), scales=bsc[:, c, :], in_=tmp["g", c][:])
+                nc.vector.quantize_mx(out=basis_codes[:, c, :].bitcast(FP8X4), scales=basis_scales[:, c, :],
+                                      in_=live["basis", c][:])
 
-        pieces = []
+        basis_work = []
         for c in range(18):
             if c % 9 in (0, 8):
-                pieces.append(("up", c))
+                basis_work.append(("up", c))
             else:
-                pieces.extend([("up", c), ("down", c), ("min", c)])
+                basis_work.extend([("up", c), ("down", c), ("min", c)])
             if c > 0:
-                pieces.append(("quant", c - 1))
+                basis_work.append(("quantise", c - 1))
             if c == 0:
-                pieces.extend([("silu", 0), ("silu", 1)])
+                basis_work.extend([("silu", 0), ("silu", 1)])
             if c == 6:
-                pieces.append(("clamp", 1))
-        pieces.append(("quant", 17))
+                basis_work.append(("clip", 1))
+        basis_work.append(("quantise", 17))
 
-        grp = {}
-        wc = {}
-        ws = {}
-        acc = {}
-        ot = {}
+        grouped = {}
+        w_codes = {}
+        w_scales = {}
+        sums = {}
+        biased = {}
 
-        def w_bank(j, on_vector):
+        def weight_bank(j, on_vector):
             t, r = divmod(j, BANKS)
-            tpw = bank("tpw")
+            turned = bank("tpw")
             for g in range(4):
-                words = wn[t][:, g, :].bitcast(F32)
-                nc.tensor.transpose(tpw[:, P * g:P * g + P], words[:, r:r + 9 * 127 + 1:9], ident_f[:])
-            grp[j] = gpool.tile([P, 1024], BF16, tag="grp", name="grp", align_bytes=64)
-            src = tpw[:].bitcast(BF16).rearrange("p (n e) -> p e n", e=2)
-            dst = grp[j][:].rearrange("p (e n) -> p e n", e=2)
+                words = raw[t][:, g, :].bitcast(F32)
+                nc.tensor.transpose(turned[:, P * g:P * g + P], words[:, r:r + 9 * 127 + 1:9], ident_f[:])
+            grouped[j] = gpool.tile([P, 1024], BF16, tag="grp", name="grp", align_bytes=64)
+            src = turned[:].bitcast(BF16).rearrange("p (n e) -> p e n", e=2)
+            dst = grouped[j][:].rearrange("p (e n) -> p e n", e=2)
             if on_vector:
                 nc.vector.tensor_copy(out=dst, in_=src)
             else:
                 nc.scalar.copy(out=dst, in_=src)
 
-        def w_quant(j):
+        def quantise_bank(j):
             t, r = divmod(j, BANKS)
             if r == 0:
-                wc[t] = cpool.tile([P, 18, P], U32, tag="wc", name="wc", align_bytes=64)
-                ws[t] = cpool.tile([P, 18, P], U8, tag="ws", name="ws", align_bytes=64)
-            nc.vector.quantize_mx(out=wc[t][:, 2 * r:2 * r + 2, :].rearrange("p c o -> p (c o)").bitcast(FP8X4),
-                                  scales=ws[t][:, 2 * r:2 * r + 2, :].rearrange("p c o -> p (c o)"), in_=grp[j][:])
+                w_codes[t] = cpool.tile([P, 18, P], U32, tag="wc", name="wc", align_bytes=64)
+                w_scales[t] = cpool.tile([P, 18, P], U8, tag="ws", name="ws", align_bytes=64)
+            nc.vector.quantize_mx(out=w_codes[t][:, 2 * r:2 * r + 2, :].rearrange("p c o -> p (c o)").bitcast(FP8X4),
+                                  scales=w_scales[t][:, 2 * r:2 * r + 2, :].rearrange("p c o -> p (c o)"),
+                                  in_=grouped[j][:])
 
-        npass = [0] * TILES
+        passes_written = [0] * TILES
 
-        def mx_pass(t, idx):
-            if npass[t] == 0:
-                acc[t] = bank("acc")
-            first = npass[t] == 0
-            last = npass[t] == 19
-            if idx < 18:
-                nc.tensor.matmul_mx(out=acc[t][:], lhsT=wc[t][:, idx, :].bitcast(FP8X4), lhsT_scale=ws[t][:, idx, :],
-                                    rhs=bc[:, idx, :].bitcast(FP8X4), rhs_scale=bsc[:, idx, :], start=first, stop=last)
+        def mx_pass(t, c):
+            if passes_written[t] == 0:
+                sums[t] = bank("acc")
+            first = passes_written[t] == 0
+            last = passes_written[t] == PASSES - 1
+            if c < 18:
+                nc.tensor.matmul_mx(out=sums[t][:], lhsT=w_codes[t][:, c, :].bitcast(FP8X4), lhsT_scale=w_scales[t][:, c, :],
+                                    rhs=basis_codes[:, c, :].bitcast(FP8X4), rhs_scale=basis_scales[:, c, :],
+                                    start=first, stop=last)
             else:
-                g = idx - 18
-                nc.tensor.matmul_mx(out=acc[t][:], lhsT=bw[:, g, 256 * t:256 * t + 256].bitcast(FP4X4),
-                                    lhsT_scale=bs[:, g, P * t:P * t + P],
-                                    rhs=scod[:, 512 * g:512 * g + 512].bitcast(FP8X4),
-                                    rhs_scale=ssc[:, 512 * g:512 * g + 512], start=first, stop=last)
-            npass[t] += 1
+                g = c - 18
+                nc.tensor.matmul_mx(out=sums[t][:], lhsT=base_words[:, g, 256 * t:256 * t + 256].bitcast(FP4X4),
+                                    lhsT_scale=base_scales[:, g, P * t:P * t + P],
+                                    rhs=silu_codes[:, 512 * g:512 * g + 512].bitcast(FP8X4),
+                                    rhs_scale=silu_scales[:, 512 * g:512 * g + 512], start=first, stop=last)
+            passes_written[t] += 1
 
         def add_bias(t):
-            ot[t] = opool.tile([P, 512], F32, tag="ot", name="ot", align_bytes=64)
-            nc.scalar.activation(out=ot[t][:], in_=acc[t][:], func=AF.Identity, bias=bcol[:, t:t + 1], scale=1.0)
+            biased[t] = opool.tile([P, 512], F32, tag="ot", bufs=3, name="ot", align_bytes=64)
+            nc.scalar.activation(out=biased[t][:], in_=sums[t][:], func=AF.Identity, bias=bias_col[:, t:t + 1], scale=1.0)
 
         def turn_and_store(t):
-            z = opool.tile([P, 512], F32, tag="z", name="z", align_bytes=64)
-            nc.vector.transpose(out=z[:], in_=ot[t][:])
+            z = opool.tile([P, 512], F32, tag="z", bufs=4, name="z", align_bytes=64)
+            nc.vector.transpose(out=z[:], in_=biased[t][:])
             rows = out.rearrange("(c w) o -> w c o", w=32)
             for a in range(4):
                 nc.sync.dma_start(out=rows[:, :, P * t + 32 * a:P * t + 32 * a + 32],
                                   in_=z[32 * a:32 * a + 32, :].rearrange("w (c r) -> w c r", r=32))
 
-        w_step = [[LATE] * 20 for t in range(TILES)]
-        b_step = [LATE] * 18
-        sent = [[False] * 20 for t in range(TILES)]
-        done_step = [LATE] * TILES
-        bias_step = [LATE] * TILES
+        w_step = [[NEVER] * PASSES for t in range(TILES)]
+        b_step = [NEVER] * 18
+        sent = [[False] * PASSES for t in range(TILES)]
+        closed_step = [NEVER] * TILES
+        bias_step = [NEVER] * TILES
         stored = [False] * TILES
-        nbank = 0
-        nquant = 0
-        npiece = 0
+        banks_written = 0
+        banks_quantised = 0
+        basis_written = 0
         step = 0
         while not all(stored):
-            assert step < 500
             for t in range(TILES):
                 if bias_step[t] < step and not stored[t]:
                     turn_and_store(t)
                     stored[t] = True
-            for t in [t for t in range(TILES) if done_step[t] < step and bias_step[t] == LATE][:2]:
+            for t in [t for t in range(TILES) if closed_step[t] < step and bias_step[t] == NEVER][:3]:
                 add_bias(t)
                 bias_step[t] = step
-            before = nbank
+            before = banks_written
             for i in range(STEP_BANKS):
-                t, r = divmod(nbank, BANKS)
-                if nbank < TILES * BANKS and (r > 0 or t < CODES or done_step[t - CODES] < LATE):
-                    w_bank(nbank, nbank % (3 if npiece >= len(pieces) else 1000) == 0)
-                    nbank += 1
+                t, r = divmod(banks_written, BANKS)
+                if banks_written < TILES * BANKS and (r > 0 or t < CODES or closed_step[t - CODES] < NEVER):
+                    basis_done = basis_written >= len(basis_work)
+                    weight_bank(banks_written, banks_written % 3 == 0 if basis_done else banks_written == 0)
+                    banks_written += 1
                     if r == BANKS - 1 and t + 2 < TILES:
-                        load_w(t + 2)
-            while nquant < before:
-                t, r = divmod(nquant, BANKS)
-                w_quant(nquant)
+                        load_weights(t + 2)
+            while banks_quantised < before:
+                t, r = divmod(banks_quantised, BANKS)
+                quantise_bank(banks_quantised)
                 w_step[t][2 * r] = step
                 w_step[t][2 * r + 1] = step
-                nquant += 1
-            for kind, c in pieces[npiece:npiece + (STEP_BASIS if nbank - before == STEP_BANKS else 2 * STEP_BASIS)]:
-                piece(kind, c)
-                if kind == "quant":
+                banks_quantised += 1
+            share = STEP_BASIS if banks_written - before == STEP_BANKS else 2 * STEP_BASIS
+            for kind, c in basis_work[basis_written:basis_written + share]:
+                basis_instruction(kind, c)
+                if kind == "quantise":
                     b_step[c] = step
                 if kind == "silu":
                     for t in range(TILES):
                         w_step[t][18 + c] = step
-                npiece += 1
+                basis_written += 1
             ready = []
             for t in range(TILES):
-                if t < OPEN or bias_step[t - OPEN] < LATE:
-                    for idx in [18, 19] + list(range(18)):
-                        if not sent[t][idx] and w_step[t][idx] < step and (idx >= 18 or b_step[idx] < step):
-                            ready.append((t, idx))
-            for t, idx in ready[:STEP_PASSES]:
-                mx_pass(t, idx)
-                sent[t][idx] = True
-                if npass[t] == 20:
-                    done_step[t] = step
+                if t < OPEN or bias_step[t - OPEN] < NEVER:
+                    for c in [18, 19] + list(range(18)):
+                        if not sent[t][c] and w_step[t][c] < step and (c >= 18 or b_step[c] < step):
+                            ready.append((t, c))
+            for t, c in ready[:STEP_PASSES]:
+                mx_pass(t, c)
+                sent[t][c] = True
+                if passes_written[t] == PASSES:
+                    closed_step[t] = step
             step += 1

from contextlib import ExitStack

import concourse.mybir as mybir
from concourse.masks import make_identity

F32 = mybir.dt.float32
BF16 = mybir.dt.bfloat16
I32 = mybir.dt.int32
U32 = mybir.dt.uint32
U8 = mybir.dt.uint8
FP8X4 = mybir.dt.float8_e4m3fn_x4
FP4X4 = mybir.dt.float4_e2m1fn_x4
ALU = mybir.AluOpType
AF = mybir.ActivationFunctionType

FLOPS = 2 * 512 * 1024 * 1024 * 10

P = 128
TILES = 8
BANKS = 9
PASSES = 20
OPEN = 5
CODES = 6
STEP_BANKS = 3
STEP_BASIS = 4
STEP_PASSES = 8
NEVER = 10 ** 6


def tile_kanbasislinear_kernel(tc, x, spline_weight, base_weight_words, base_weight_scales, bias, out):
    nc = tc.nc
    with ExitStack() as ctx:
        const = ctx.enter_context(tc.tile_pool(name="const", bufs=1))
        work = ctx.enter_context(tc.tile_pool(name="work", bufs=1))
        wnat = ctx.enter_context(tc.tile_pool(name="wnat", bufs=2))
        gpool = ctx.enter_context(tc.tile_pool(name="gpool", bufs=8))
        cpool = ctx.enter_context(tc.tile_pool(name="cpool", bufs=CODES))
        opool = ctx.enter_context(tc.tile_pool(name="opool", bufs=2))
        psum = ctx.enter_context(tc.psum_pool(name="psum", bufs=8))

        def bank(name):
            return psum.tile([P, 512], F32, tag="bank", name=name)

        warm = const.tile([P, 2], F32, name="warm")
        nc.vector.memset(warm[:], 0.0)
        nc.scalar.activation(out=warm[:, 1:2], in_=warm[:, 0:1], func=AF.Silu)
        x_sb = wnat.tile([P, 4, 1024], BF16, tag="wn", name="x_sb")
        for bt in range(4):
            nc.sync.dma_start(out=x_sb[:, bt, :], in_=x[P * bt:P * bt + P, :])
        ident_f = const.tile([P, P], F32, name="ident_f")
        make_identity(nc, ident_f[:])
        ident_b = const.tile([P, P], BF16, name="ident_b")
        make_identity(nc, ident_b[:])
        bias_rows = const.tile([P, P], BF16, name="brow")
        nc.vector.memset(bias_rows[:], 0.0)
        base_scales = const.tile([P, 2, 1024], U8, name="bs", align_bytes=64)
        nc.vector.memset(base_scales[:].bitcast(I32), 0)
        base_words = const.tile([P, 2, 2048], U8, name="bw", align_bytes=64)
        nc.sync.dma_start(out=bias_rows[0:8, :], in_=bias.rearrange("(t p) -> t p", p=P))
        raw = {}

        def load_weights(t):
            raw[t] = wnat.tile([P, 4, 2304], BF16, tag="wn", name="wn")
            quarters = spline_weight[P * t:P * t + P].rearrange("o (u m) k -> (o u) (m k)", u=4)
            nc.sync.dma_start(out=raw[t][:], in_=quarters.rearrange("(g q) w -> q g w", q=P))

        load_weights(0)
        scale_rows = base_weight_scales.rearrange("g q n -> q g n")
        for r in range(4):
            nc.sync.dma_start(out=base_scales[r:P:32, :, :].bitcast(I32), in_=scale_rows[r:16:4].bitcast(I32))
        nc.sync.dma_start(out=base_words[:].bitcast(I32), in_=base_weight_words.rearrange("g p n -> p g n").bitcast(I32))

        x_words = x_sb[:].bitcast(F32)
        twice_x = cpool.tile([P, 2, 512, 4], BF16, tag="wc", name="xp", align_bytes=64)
        for bt in range(4):
            turned = bank("tpx")
            for u in range(4):
                nc.tensor.transpose(turned[:, P * u:P * u + P], x_words[:, bt, P * u:P * u + P], ident_f[:])
            src = turned[:].bitcast(BF16).rearrange("p (u b e) -> p e b u", u=4, b=P, e=2)
            dst = twice_x[:, :, P * bt:P * bt + P, :]
            if bt < 2:
                nc.scalar.activation(out=dst, in_=src, func=AF.Copy, scale=2.0)
            else:
                nc.vector.tensor_scalar(out=dst, in0=src, scalar1=2.0, scalar2=None, op0=ALU.mult)
        pos = const.tile([P, 4096], BF16, name="xs")
        neg = const.tile([P, 4096], BF16, name="nxs")

        def clip(h):
            half = slice(2048 * h, 2048 * h + 2048)
            nc.vector.tensor_scalar(out=pos[:, half], in0=twice_x[:, h].rearrange("p b u -> p (b u)"), scalar1=-4.0,
                                    scalar2=4.0, op0=ALU.max, op1=ALU.min)
            nc.vector.tensor_scalar(out=neg[:, half], in0=pos[:, half], scalar1=-1.0, scalar2=None, op0=ALU.mult)

        clip(0)

        silu = [work.tile([P, 512, 4], BF16, tag="bg", bufs=3, name="sg", align_bytes=64) for g in range(2)]
        for bt in range(4):
            turned = bank("tps")
            for g in range(2):
                for v in range(2):
                    nc.tensor.transpose(turned[:, P * (2 * g + v):P * (2 * g + v) + P],
                                        x_words[:, bt, 256 * g + v:256 * (g + 1):2], ident_f[:])
            pairs = turned[:].bitcast(BF16).rearrange("p (g v b e) -> p g b v e", g=2, v=2, b=P, e=2)
            for g in range(2):
                nc.scalar.activation(out=silu[g][:, P * bt:P * bt + P, :].rearrange("p b (v e) -> p b v e", v=2, e=2),
                                     in_=pairs[:, g], func=AF.Silu)
        turned_bias = psum.tile([P, P], BF16, tag="bank", name="tpb")
        nc.tensor.transpose(turned_bias[:], bias_rows[:], ident_b[:])
        bias_col = const.tile([P, 8], F32, name="bcol")
        nc.vector.tensor_copy(out=bias_col[:], in_=turned_bias[:, 0:8])
        silu_codes = const.tile([P, 1024], U32, name="scod", align_bytes=64)
        silu_scales = const.tile([P, 1024], U8, name="ssc", align_bytes=64)
        load_weights(1)

        basis_codes = const.tile([P, 18, 512], U32, name="bc", align_bytes=64)
        basis_scales = const.tile([P, 18, 512], U8, name="bsc", align_bytes=64)
        live = {}

        def new_basis(c):
            live["basis", c] = work.tile([P, 2048], BF16, tag="bg", bufs=3, name="bg", align_bytes=64)
            return live["basis", c]

        def ramp(dst, src, h, shift):
            nc.vector.tensor_scalar(out=dst[:], in0=src[:, 2048 * h:2048 * h + 2048], scalar1=float(shift), scalar2=0.0,
                                    op0=ALU.add, op1=ALU.max)

        def basis_instruction(kind, c):
            h, k = divmod(c, 9)
            if kind == "clip":
                clip(c)
            elif kind == "silu":
                nc.vector.quantize_mx(out=silu_codes[:, 512 * c:512 * c + 512].bitcast(FP8X4),
                                      scales=silu_scales[:, 512 * c:512 * c + 512],
                                      in_=silu[c][:].rearrange("p b t -> p (b t)"))
            elif kind == "up":
                if k == 0:
                    ramp(new_basis(c), neg, h, -3)
                elif k == 8:
                    ramp(new_basis(c), pos, h, -3)
                else:
                    live["up"] = work.tile([P, 2048], BF16, tag="ra", name="ra")
                    ramp(live["up"], pos, h, 5 - k)
            elif kind == "down":
                live["down"] = work.tile([P, 2048], BF16, tag="rb", name="rb")
                ramp(live["down"], neg, h, k - 3)
            elif kind == "min":
                nc.vector.tensor_tensor(out=new_basis(c)[:], in0=live["up"][:], in1=live["down"][:], op=ALU.min)
            else:
                nc.vector.quantize_mx(out=basis_codes[:, c, :].bitcast(FP8X4), scales=basis_scales[:, c, :],
                                      in_=live["basis", c][:])

        basis_work = []
        for c in range(18):
            if c % 9 in (0, 8):
                basis_work.append(("up", c))
            else:
                basis_work.extend([("up", c), ("down", c), ("min", c)])
            if c > 0:
                basis_work.append(("quantise", c - 1))
            if c == 0:
                basis_work.extend([("silu", 0), ("silu", 1)])
            if c == 6:
                basis_work.append(("clip", 1))
        basis_work.append(("quantise", 17))

        grouped = {}
        w_codes = {}
        w_scales = {}
        sums = {}
        biased = {}

        def weight_bank(j, on_vector):
            t, r = divmod(j, BANKS)
            turned = bank("tpw")
            for g in range(4):
                words = raw[t][:, g, :].bitcast(F32)
                nc.tensor.transpose(turned[:, P * g:P * g + P], words[:, r:r + 9 * 127 + 1:9], ident_f[:])
            grouped[j] = gpool.tile([P, 1024], BF16, tag="grp", name="grp", align_bytes=64)
            src = turned[:].bitcast(BF16).rearrange("p (n e) -> p e n", e=2)
            dst = grouped[j][:].rearrange("p (e n) -> p e n", e=2)
            if on_vector:
                nc.vector.tensor_copy(out=dst, in_=src)
            else:
                nc.scalar.copy(out=dst, in_=src)

        def quantise_bank(j):
            t, r = divmod(j, BANKS)
            if r == 0:
                w_codes[t] = cpool.tile([P, 18, P], U32, tag="wc", name="wc", align_bytes=64)
                w_scales[t] = cpool.tile([P, 18, P], U8, tag="ws", name="ws", align_bytes=64)
            nc.vector.quantize_mx(out=w_codes[t][:, 2 * r:2 * r + 2, :].rearrange("p c o -> p (c o)").bitcast(FP8X4),
                                  scales=w_scales[t][:, 2 * r:2 * r + 2, :].rearrange("p c o -> p (c o)"),
                                  in_=grouped[j][:])

        passes_written = [0] * TILES

        def mx_pass(t, c):
            if passes_written[t] == 0:
                sums[t] = bank("acc")
            first = passes_written[t] == 0
            last = passes_written[t] == PASSES - 1
            if c < 18:
                nc.tensor.matmul_mx(out=sums[t][:], lhsT=w_codes[t][:, c, :].bitcast(FP8X4), lhsT_scale=w_scales[t][:, c, :],
                                    rhs=basis_codes[:, c, :].bitcast(FP8X4), rhs_scale=basis_scales[:, c, :],
                                    start=first, stop=last)
            else:
                g = c - 18
                nc.tensor.matmul_mx(out=sums[t][:], lhsT=base_words[:, g, 256 * t:256 * t + 256].bitcast(FP4X4),
                                    lhsT_scale=base_scales[:, g, P * t:P * t + P],
                                    rhs=silu_codes[:, 512 * g:512 * g + 512].bitcast(FP8X4),
                                    rhs_scale=silu_scales[:, 512 * g:512 * g + 512], start=first, stop=last)
            passes_written[t] += 1

        def add_bias(t):
            biased[t] = opool.tile([P, 512], F32, tag="ot", bufs=3, name="ot", align_bytes=64)
            nc.scalar.activation(out=biased[t][:], in_=sums[t][:], func=AF.Identity, bias=bias_col[:, t:t + 1], scale=1.0)

        def turn_and_store(t):
            z = opool.tile([P, 512], F32, tag="z", bufs=4, name="z", align_bytes=64)
            nc.vector.transpose(out=z[:], in_=biased[t][:])
            rows = out.rearrange("(c w) o -> w c o", w=32)
            for a in range(4):
                nc.sync.dma_start(out=rows[:, :, P * t + 32 * a:P * t + 32 * a + 32],
                                  in_=z[32 * a:32 * a + 32, :].rearrange("w (c r) -> w c r", r=32))

        w_step = [[NEVER] * PASSES for t in range(TILES)]
        b_step = [NEVER] * 18
        sent = [[False] * PASSES for t in range(TILES)]
        closed_step = [NEVER] * TILES
        bias_step = [NEVER] * TILES
        stored = [False] * TILES
        banks_written = 0
        banks_quantised = 0
        basis_written = 0
        step = 0
        while not all(stored):
            for t in range(TILES):
                if bias_step[t] < step and not stored[t]:
                    turn_and_store(t)
                    stored[t] = True
            for t in [t for t in range(TILES) if closed_step[t] < step and bias_step[t] == NEVER][:3]:
                add_bias(t)
                bias_step[t] = step
            before = banks_written
            for i in range(STEP_BANKS):
                t, r = divmod(banks_written, BANKS)
                if banks_written < TILES * BANKS and (r > 0 or t < CODES or closed_step[t - CODES] < NEVER):
                    basis_done = basis_written >= len(basis_work)
                    weight_bank(banks_written, banks_written % 3 == 0 if basis_done else banks_written == 0)
                    banks_written += 1
                    if r == BANKS - 1 and t + 2 < TILES:
                        load_weights(t + 2)
            while banks_quantised < before:
                t, r = divmod(banks_quantised, BANKS)
                quantise_bank(banks_quantised)
                w_step[t][2 * r] = step
                w_step[t][2 * r + 1] = step
                banks_quantised += 1
            share = STEP_BASIS if banks_written - before == STEP_BANKS else 2 * STEP_BASIS
            for kind, c in basis_work[basis_written:basis_written + share]:
                basis_instruction(kind, c)
                if kind == "quantise":
                    b_step[c] = step
                if kind == "silu":
                    for t in range(TILES):
                        w_step[t][18 + c] = step
                basis_written += 1
            ready = []
            for t in range(TILES):
                if t < OPEN or bias_step[t - OPEN] < NEVER:
                    for c in [18, 19] + list(range(18)):
                        if not sent[t][c] and w_step[t][c] < step and (c >= 18 or b_step[c] < step):
                            ready.append((t, c))
            for t, c in ready[:STEP_PASSES]:
                mx_pass(t, c)
                sent[t][c] = True
                if passes_written[t] == PASSES:
                    closed_step[t] = step
            step += 1
